import numpy as np
import ml_dtypes


def mxq(x, axis, fmt="e4m3"):
    dtype, down = {"e4m3": (ml_dtypes.float8_e4m3fn, 7), "e5m2": (ml_dtypes.float8_e5m2, 14)}[fmt]
    v = np.moveaxis(np.asarray(x, np.float32).astype(ml_dtypes.bfloat16).astype(np.float64), axis, -1)
    blocks = v.reshape(v.shape[:-1] + (-1, 32))
    amax = np.abs(blocks).max(-1, keepdims=True)
    byte = np.maximum(np.where(amax > 0, np.frexp(amax)[1] - 1 + 127, 0) - down, 1)
    scale = np.exp2(byte - 127.0)
    codes = (blocks / scale).astype(np.float32).astype(dtype).astype(np.float64)
    return np.moveaxis((codes * scale).reshape(v.shape), -1, axis)


WIDE = False


def mx_kscale(k):
    if not WIDE:
        return np.ones(k)
    levels = np.array([10, -10, 5, -5, 0])
    a = np.random.permutation(np.resize(levels, k // 512 * 4)).reshape(k // 512, 4)
    idx = np.arange(k)
    return np.exp2(a[idx // 512, idx % 128 // 32])


BF16 = ml_dtypes.bfloat16


def bf(x):
    return np.asarray(x, np.float32).astype(BF16)


def f64(x):
    return np.asarray(x).astype(np.float64)


E2M1 = np.array([0.0, 0.5, 1.0, 1.5, 2.0, 3.0, 4.0, 6.0, -0.0, -0.5, -1.0, -1.5, -2.0, -3.0, -4.0, -6.0])


def pack_weight(w, fmt):
    k, n = w.shape
    w = f64(bf(w)).reshape(k // 32, 32, n)
    amax = np.abs(w).max(1)
    if fmt == "e4m3":
        byte = np.frexp(amax)[1] - 1 + 127 - 7
    else:
        mant, ex = np.frexp(amax / 6.0)
        byte = np.where(mant > 0.5, ex, ex - 1) + 127
    byte = np.clip(np.where(amax > 0, byte, 1), 1, 254)
    scaled = (w * np.exp2(127.0 - byte)[:, None, :]).reshape(k, n).astype(np.float32)
    by_word = np.ascontiguousarray(scaled.reshape(k // 512, 128, 4, n).transpose(0, 1, 3, 2))
    if fmt == "e4m3":
        words = by_word.astype(ml_dtypes.float8_e4m3fn).view(np.uint8)
    else:
        c = by_word.astype(ml_dtypes.float4_e2m1fn).view(np.uint8) & 0xF
        words = c[..., 0::2] | (c[..., 1::2] << 4)
    return np.ascontiguousarray(words), np.ascontiguousarray(byte.astype(np.uint8).reshape(k // 512, 16, n))


def unpack_weight(words, scales, fmt):
    g, p, n, _ = words.shape
    if fmt == "e4m3":
        vals = np.ascontiguousarray(words).view(ml_dtypes.float8_e4m3fn).astype(np.float64)
    else:
        nib = np.empty((g, p, n, 4), np.uint8)
        nib[..., 0::2] = words & 0xF
        nib[..., 1::2] = words >> 4
        vals = E2M1[nib]
    vals = vals * np.repeat(np.exp2(scales.astype(np.float64) - 127.0), 8, axis=1)[..., None]
    return vals.transpose(0, 1, 3, 2).reshape(g * 512, n)

def pack4(w):
    words, scales = pack_weight(w, "e2m1")
    return words.reshape(words.shape[0], 128, -1), scales


def unpack4(words, scales):
    return unpack_weight(words.reshape(words.shape[0], 128, -1, 2), scales, "e2m1")


B, NH, T, D, N, CK = 1, 6, 1024, 512, 256, 512
KD = NH * N
EPS_LN = 1e-5
TARGET_ACTIVITY = 0.1


def layernorm(v):
    m = np.mean(v, axis=-1, keepdims=True)
    var = np.mean((v - m) ** 2, axis=-1, keepdims=True)
    return (v - m) / np.sqrt(var + EPS_LN)


def setup_inputs():
    t = mx_kscale(KD)
    xy = np.maximum(np.random.standard_normal((B, NH, T, N)) * 0.5, 0.0) * np.maximum(np.random.standard_normal((B, NH, T, N)), 0.0)
    xy_sparse = bf(xy * t.reshape(NH, 1, N))
    decoder_words, decoder_scales = pack4(np.random.standard_normal((KD, D)) * 2.0 / np.sqrt(KD) / t[:, None])
    return {'xy_sparse': xy_sparse,
            'decoder_words': decoder_words,
            'decoder_scales': decoder_scales,
            'x': bf(np.random.standard_normal((B, 1, T, D))),
            'scale': bf(1.0 + 0.1 * np.random.standard_normal(D)),
            'running_activity': bf(TARGET_ACTIVITY * np.exp(0.5 * np.random.standard_normal(D)))}


def reference(xy_sparse, decoder_words, decoder_scales, x, scale, running_activity):
    flat = f64(xy_sparse).transpose(0, 2, 1, 3).reshape(B, 1, T, KD)
    y_mlp = mxq(flat, 3, 'e4m3') @ unpack4(decoder_words, decoder_scales)
    y = layernorm(y_mlp)
    regulation = TARGET_ACTIVITY / (f64(running_activity) + 1e-6)
    y = y * np.sqrt(regulation) * f64(scale)
    return layernorm(f64(x) + y)

@@ -1,0 +1,271 @@
+from contextlib import ExitStack
+
+import concourse.mybir as mybir
+from concourse.masks import make_identity
+
+F32 = mybir.dt.float32
+BF16 = mybir.dt.bfloat16
+I32 = mybir.dt.int32
+U32 = mybir.dt.uint32
+U8 = mybir.dt.uint8
+FP8X4 = mybir.dt.float8_e4m3fn_x4
+FP4X4 = mybir.dt.float4_e2m1fn_x4
+ALU = mybir.AluOpType
+ACT = mybir.ActivationFunctionType
+
+P = 128
+HEADS = 6
+HEAD_DIM = 256
+TOKENS = 1024
+D = 512
+K_PASS = 512
+PASSES = HEADS * HEAD_DIM // K_PASS
+TILES = TOKENS // P
+PAIRS = TILES // 2
+UNITS = 2 * PASSES
+BANKS = UNITS // 2
+WORDS = K_PASS // 2
+EPS_LN = 1e-5
+TARGET_ACTIVITY = 0.1
+
+FLOPS = 2 * TOKENS * HEADS * HEAD_DIM * D
+
+
+def tile_bdhlayer_pc_kernel(
+    tc, xy_sparse, decoder_words, decoder_scales, x, scale, running_activity, out
+):
+    nc = tc.nc
+    xy_tiles = xy_sparse.rearrange("b h (p j) n -> j p (b h) n", j=TILES)
+    x_rows = x.rearrange("a b (p j) n -> p (a b j) n", j=TILES)
+    out_rows = out.rearrange("a b (p j) n -> p (a b j) n", j=TILES)
+
+    with ExitStack() as ctx:
+        keep = ctx.enter_context(tc.tile_pool(name="keep", bufs=1))
+        stage = ctx.enter_context(tc.tile_pool(name="stage", bufs=2))
+        work = ctx.enter_context(tc.tile_pool(name="work", bufs=4))
+        small = ctx.enter_context(tc.tile_pool(name="small", bufs=4))
+        psum_t = ctx.enter_context(tc.psum_pool(name="psum_t", bufs=BANKS))
+        psum_acc = ctx.enter_context(tc.psum_pool(name="psum_acc", bufs=4))
+        ctx.enter_context(tc.manual_schedule())
+
+        w_planes = keep.tile([P, PASSES, D], U8, align_bytes=64)
+        nc.vector.memset(w_planes[:].bitcast(I32), 0)
+        vectors = keep.tile([P, 2 * D], BF16)
+        nc.vector.memset(vectors[:], 0.0)
+        ones = keep.tile([P, P], BF16)
+        nc.vector.memset(ones[:], 1.0)
+        ident = keep.tile([P, P], F32)
+        make_identity(nc, ident[:])
+
+        nc.scalar.dma_start(out=vectors[0:1, 0:D], in_=scale.unsqueeze(0))
+        nc.scalar.dma_start(out=vectors[0:1, D : 2 * D], in_=running_activity.unsqueeze(0))
+
+        xs = []
+        for j in range(TILES):
+            xs.append(keep.tile([P, HEADS * HEAD_DIM], BF16, name="xs%d" % j))
+        x_in = []
+        for i in range(PAIRS):
+            x_in.append(keep.tile([P, 2, D], BF16, name="x_in%d" % i))
+        w_words = keep.tile([P, PASSES, 2 * D], U8, align_bytes=64)
+
+        def load_xy(j):
+            nc.sync.dma_start(
+                out=xs[j][:].rearrange("p (h n) -> p h n", h=HEADS), in_=xy_tiles[j]
+            )
+
+        def load_x(i):
+            nc.sync.dma_start(out=x_in[i][:], in_=x_rows[:, 2 * i : 2 * i + 2, :])
+
+        load_xy(0)
+        load_xy(1)
+        for q in range(4):
+            nc.sync.dma_start(
+                out=w_planes[32 * q : 32 * q + 4].bitcast(I32),
+                in_=decoder_scales.bitcast(I32)[:, 4 * q : 4 * q + 4, :].rearrange(
+                    "g r w -> r g w"
+                ),
+            )
+        nc.sync.dma_start(
+            out=w_words[:].bitcast(I32),
+            in_=decoder_words.bitcast(I32).rearrange("g p w -> p g w"),
+        )
+        for i in range(1, PAIRS):
+            load_xy(2 * i)
+            load_xy(2 * i + 1)
+            load_x(i - 1)
+        load_x(PAIRS - 1)
+
+        banks = {}
+        codes = {}
+        planes = {}
+        acc = {}
+        mean_var = {}
+        rstd1 = {}
+        centred = {}
+        summed = {}
+        z_sum = {}
+        neg_mean2 = {}
+        rstd2 = {}
+
+        def transposes(i):
+            for b in range(BANKS):
+                xt = psum_t.tile([P, 2, 2, P], F32, name="xt")
+                banks[(i, b)] = xt
+                for s in range(2):
+                    n = 2 * b + s
+                    words = xs[2 * i + n // PASSES][:].bitcast(F32)
+                    g = n % PASSES
+                    for u in range(2):
+                        nc.tensor.transpose(
+                            xt[:, s, u, :],
+                            words[:, WORDS * g + u : WORDS * (g + 1) : 2],
+                            ident[:],
+                        )
+
+        def quantise(i):
+            grouped = stage.tile([P, UNITS * K_PASS], BF16, align_bytes=64, name="grouped")
+            codes[i] = stage.tile([P, UNITS * P], U32, align_bytes=64, name="codes")
+            planes[i] = stage.tile([P, UNITS * P], U8, align_bytes=64, name="planes")
+            for b in range(BANKS):
+                nc.scalar.copy(
+                    out=grouped[:]
+                    .bitcast(F32)[:, 2 * WORDS * b : 2 * WORDS * (b + 1)]
+                    .rearrange("p (s r u) -> p s r u", s=2, u=2),
+                    in_=banks[(i, b)][:].rearrange("p s u r -> p s r u"),
+                )
+            for b in range(BANKS):
+                nc.vector.quantize_mx(
+                    out=codes[i][:, 2 * P * b : 2 * P * (b + 1)].bitcast(FP8X4),
+                    scales=planes[i][:, 2 * P * b : 2 * P * (b + 1)],
+                    in_=grouped[:, 2 * K_PASS * b : 2 * K_PASS * (b + 1)],
+                )
+
+        def multiply(i):
+            for t in range(2):
+                j = 2 * i + t
+                acc[j] = psum_acc.tile([P, D], F32, name="acc")
+                for g in range(PASSES):
+                    n = PASSES * t + g
+                    nc.tensor.matmul_mx(
+                        out=acc[j][:],
+                        lhsT=codes[i][:, P * n : P * (n + 1)].bitcast(FP8X4),
+                        lhsT_scale=planes[i][:, P * n : P * (n + 1)],
+                        rhs=w_words[:, g, :].bitcast(FP4X4),
+                        rhs_scale=w_planes[:, g, :],
+                        start=(g == 0),
+                        stop=(g == PASSES - 1),
+                    )
+
+        def first_stats(i):
+            stats = {}
+            for j in (2 * i, 2 * i + 1):
+                stats[j] = small.tile([P, 6], F32, name="stats")
+                nc.vector.bn_stats(out=stats[j][:], in_=acc[j][:])
+            for j in (2 * i, 2 * i + 1):
+                mean_var[j] = small.tile([P, 2], F32, name="mean_var")
+                nc.vector.bn_aggr(out=mean_var[j][:], in_=stats[j][:])
+                rstd1[j] = small.tile([P, 1], F32, name="rstd1")
+                nc.scalar.activation(
+                    out=rstd1[j][:],
+                    in_=mean_var[j][:, 1:2],
+                    func=ACT.Abs_reciprocal_sqrt,
+                    bias=EPS_LN,
+                    scale=1.0,
+                )
+
+        def centre_and_gain(i):
+            for j in (2 * i, 2 * i + 1):
+                centred[j] = work.tile([P, D], F32, name="centred")
+                nc.vector.scalar_tensor_tensor(
+                    out=centred[j][:],
+                    in0=acc[j][:],
+                    scalar=mean_var[j][:, 0:1],
+                    in1=gain[:],
+                    op0=ALU.subtract,
+                    op1=ALU.mult,
+                )
+
+        def add_tokens(i):
+            for t in range(2):
+                j = 2 * i + t
+                summed[j] = work.tile([P, D], F32, name="summed")
+                z_sum[j] = small.tile([P, 1], F32, name="z_sum")
+                nc.vector.scalar_tensor_tensor(
+                    out=summed[j][:],
+                    in0=centred[j][:],
+                    scalar=rstd1[j][:, 0:1],
+                    in1=x_in[i][:, t, :],
+                    op0=ALU.mult,
+                    op1=ALU.add,
+                    accum_out=z_sum[j][:],
+                )
+
+        def second_stats(i):
+            for j in (2 * i, 2 * i + 1):
+                neg_mean2[j] = small.tile([P, 1], F32, name="neg_mean2")
+                nc.scalar.mul(out=neg_mean2[j][:], in_=z_sum[j][:], mul=-1.0 / D)
+                squares = work.tile([P, D], BF16, name="squares")
+                sq_sum = small.tile([P, 1], F32, name="sq_sum")
+                nc.scalar.activation(
+                    out=squares[:],
+                    in_=summed[j][:],
+                    func=ACT.Square,
+                    bias=neg_mean2[j][:, 0:1],
+                    scale=1.0,
+                    accum_out=sq_sum[:],
+                )
+                rstd2[j] = small.tile([P, 1], F32, name="rstd2")
+                nc.scalar.activation(
+                    out=rstd2[j][:],
+                    in_=sq_sum[:],
+                    func=ACT.Abs_reciprocal_sqrt,
+                    bias=EPS_LN,
+                    scale=1.0 / D,
+                )
+
+        def normalise_and_store(i):
+            for j in (2 * i, 2 * i + 1):
+                result = work.tile([P, D], F32, name="result")
+                nc.vector.tensor_scalar(
+                    out=result[:],
+                    in0=summed[j][:],
+                    scalar1=neg_mean2[j][:, 0:1],
+                    scalar2=rstd2[j][:, 0:1],
+                    op0=ALU.add,
+                    op1=ALU.mult,
+                )
+                nc.sync.dma_start(out=out_rows[:, j, :], in_=result[:])
+
+        transposes(0)
+        quantise(0)
+
+        scale_rows = psum_acc.tile([P, D], F32, name="acc")
+        nc.tensor.matmul(scale_rows[:], lhsT=ones[:], rhs=vectors[:, 0:D], start=True, stop=True)
+        activity_rows = psum_acc.tile([P, D], F32, name="acc")
+        nc.tensor.matmul(
+            activity_rows[:], lhsT=ones[:], rhs=vectors[:, D : 2 * D], start=True, stop=True
+        )
+        regulation = keep.tile([P, D], F32)
+        nc.scalar.activation(
+            out=regulation[:],
+            in_=activity_rows[:],
+            func=ACT.Abs_reciprocal_sqrt,
+            bias=1e-6 / TARGET_ACTIVITY,
+            scale=1.0 / TARGET_ACTIVITY,
+        )
+        gain = keep.tile([P, D], F32)
+        nc.vector.tensor_tensor(out=gain[:], in0=regulation[:], in1=scale_rows[:], op=ALU.mult)
+
+        for i in range(PAIRS):
+            multiply(i)
+            if i + 1 < PAIRS:
+                transposes(i + 1)
+            first_stats(i)
+            if i > 0:
+                normalise_and_store(i - 1)
+            centre_and_gain(i)
+            if i + 1 < PAIRS:
+                quantise(i + 1)
+            add_tokens(i)
+            second_stats(i)
+        normalise_and_store(PAIRS - 1)

@@ -21,10 +21,8 @@ D = 512
 K_PASS = 512
 PASSES = HEADS * HEAD_DIM // K_PASS
 TILES = TOKENS // P
-PAIRS = TILES // 2
-UNITS = 2 * PASSES
-BANKS = UNITS // 2
 WORDS = K_PASS // 2
+BANK_SPLIT = ((0, 2), (2, 1))
 EPS_LN = 1e-5
 TARGET_ACTIVITY = 0.1
 
@@ -41,17 +39,17 @@ def tile_bdhlayer_pc_kernel(
 
     with ExitStack() as ctx:
         keep = ctx.enter_context(tc.tile_pool(name="keep", bufs=1))
-        stage = ctx.enter_context(tc.tile_pool(name="stage", bufs=2))
+        stage = ctx.enter_context(tc.tile_pool(name="stage", bufs=3))
         work = ctx.enter_context(tc.tile_pool(name="work", bufs=4))
         small = ctx.enter_context(tc.tile_pool(name="small", bufs=4))
-        psum_t = ctx.enter_context(tc.psum_pool(name="psum_t", bufs=BANKS))
-        psum_acc = ctx.enter_context(tc.psum_pool(name="psum_acc", bufs=4))
+        psum_t = ctx.enter_context(tc.psum_pool(name="psum_t", bufs=2))
+        psum_acc = ctx.enter_context(tc.psum_pool(name="psum_acc", bufs=3))
         ctx.enter_context(tc.manual_schedule())
 
-        w_planes = keep.tile([P, PASSES, D], U8, align_bytes=64)
-        nc.vector.memset(w_planes[:].bitcast(I32), 0)
         vectors = keep.tile([P, 2 * D], BF16)
         nc.vector.memset(vectors[:], 0.0)
+        w_planes = keep.tile([P, PASSES, D], U8, align_bytes=64)
+        nc.vector.memset(w_planes[:].bitcast(I32), 0)
         ones = keep.tile([P, P], BF16)
         nc.vector.memset(ones[:], 1.0)
         ident = keep.tile([P, P], F32)
@@ -64,7 +62,7 @@ def tile_bdhlayer_pc_kernel(
         for j in range(TILES):
             xs.append(keep.tile([P, HEADS * HEAD_DIM], BF16, name="xs%d" % j))
         x_in = []
-        for i in range(PAIRS):
+        for i in range(TILES // 2):
             x_in.append(keep.tile([P, 2, D], BF16, name="x_in%d" % i))
         w_words = keep.tile([P, PASSES, 2 * D], U8, align_bytes=64)
 
@@ -89,155 +87,11 @@ def tile_bdhlayer_pc_kernel(
             out=w_words[:].bitcast(I32),
             in_=decoder_words.bitcast(I32).rearrange("g p w -> p g w"),
         )
-        for i in range(1, PAIRS):
+        for i in range(1, TILES // 2):
             load_xy(2 * i)
-            load_xy(2 * i + 1)
             load_x(i - 1)
-        load_x(PAIRS - 1)
-
-        banks = {}
-        codes = {}
-        planes = {}
-        acc = {}
-        mean_var = {}
-        rstd1 = {}
-        centred = {}
-        summed = {}
-        z_sum = {}
-        neg_mean2 = {}
-        rstd2 = {}
-
-        def transposes(i):
-            for b in range(BANKS):
-                xt = psum_t.tile([P, 2, 2, P], F32, name="xt")
-                banks[(i, b)] = xt
-                for s in range(2):
-                    n = 2 * b + s
-                    words = xs[2 * i + n // PASSES][:].bitcast(F32)
-                    g = n % PASSES
-                    for u in range(2):
-                        nc.tensor.transpose(
-                            xt[:, s, u, :],
-                            words[:, WORDS * g + u : WORDS * (g + 1) : 2],
-                            ident[:],
-                        )
-
-        def quantise(i):
-            grouped = stage.tile([P, UNITS * K_PASS], BF16, align_bytes=64, name="grouped")
-            codes[i] = stage.tile([P, UNITS * P], U32, align_bytes=64, name="codes")
-            planes[i] = stage.tile([P, UNITS * P], U8, align_bytes=64, name="planes")
-            for b in range(BANKS):
-                nc.scalar.copy(
-                    out=grouped[:]
-                    .bitcast(F32)[:, 2 * WORDS * b : 2 * WORDS * (b + 1)]
-                    .rearrange("p (s r u) -> p s r u", s=2, u=2),
-                    in_=banks[(i, b)][:].rearrange("p s u r -> p s r u"),
-                )
-            for b in range(BANKS):
-                nc.vector.quantize_mx(
-                    out=codes[i][:, 2 * P * b : 2 * P * (b + 1)].bitcast(FP8X4),
-                    scales=planes[i][:, 2 * P * b : 2 * P * (b + 1)],
-                    in_=grouped[:, 2 * K_PASS * b : 2 * K_PASS * (b + 1)],
-                )
-
-        def multiply(i):
-            for t in range(2):
-                j = 2 * i + t
-                acc[j] = psum_acc.tile([P, D], F32, name="acc")
-                for g in range(PASSES):
-                    n = PASSES * t + g
-                    nc.tensor.matmul_mx(
-                        out=acc[j][:],
-                        lhsT=codes[i][:, P * n : P * (n + 1)].bitcast(FP8X4),
-                        lhsT_scale=planes[i][:, P * n : P * (n + 1)],
-                        rhs=w_words[:, g, :].bitcast(FP4X4),
-                        rhs_scale=w_planes[:, g, :],
-                        start=(g == 0),
-                        stop=(g == PASSES - 1),
-                    )
-
-        def first_stats(i):
-            stats = {}
-            for j in (2 * i, 2 * i + 1):
-                stats[j] = small.tile([P, 6], F32, name="stats")
-                nc.vector.bn_stats(out=stats[j][:], in_=acc[j][:])
-            for j in (2 * i, 2 * i + 1):
-                mean_var[j] = small.tile([P, 2], F32, name="mean_var")
-                nc.vector.bn_aggr(out=mean_var[j][:], in_=stats[j][:])
-                rstd1[j] = small.tile([P, 1], F32, name="rstd1")
-                nc.scalar.activation(
-                    out=rstd1[j][:],
-                    in_=mean_var[j][:, 1:2],
-                    func=ACT.Abs_reciprocal_sqrt,
-                    bias=EPS_LN,
-                    scale=1.0,
-                )
-
-        def centre_and_gain(i):
-            for j in (2 * i, 2 * i + 1):
-                centred[j] = work.tile([P, D], F32, name="centred")
-                nc.vector.scalar_tensor_tensor(
-                    out=centred[j][:],
-                    in0=acc[j][:],
-                    scalar=mean_var[j][:, 0:1],
-                    in1=gain[:],
-                    op0=ALU.subtract,
-                    op1=ALU.mult,
-                )
-
-        def add_tokens(i):
-            for t in range(2):
-                j = 2 * i + t
-                summed[j] = work.tile([P, D], F32, name="summed")
-                z_sum[j] = small.tile([P, 1], F32, name="z_sum")
-                nc.vector.scalar_tensor_tensor(
-                    out=summed[j][:],
-                    in0=centred[j][:],
-                    scalar=rstd1[j][:, 0:1],
-                    in1=x_in[i][:, t, :],
-                    op0=ALU.mult,
-                    op1=ALU.add,
-                    accum_out=z_sum[j][:],
-                )
-
-        def second_stats(i):
-            for j in (2 * i, 2 * i + 1):
-                neg_mean2[j] = small.tile([P, 1], F32, name="neg_mean2")
-                nc.scalar.mul(out=neg_mean2[j][:], in_=z_sum[j][:], mul=-1.0 / D)
-                squares = work.tile([P, D], BF16, name="squares")
-                sq_sum = small.tile([P, 1], F32, name="sq_sum")
-                nc.scalar.activation(
-                    out=squares[:],
-                    in_=summed[j][:],
-                    func=ACT.Square,
-                    bias=neg_mean2[j][:, 0:1],
-                    scale=1.0,
-                    accum_out=sq_sum[:],
-                )
-                rstd2[j] = small.tile([P, 1], F32, name="rstd2")
-                nc.scalar.activation(
-                    out=rstd2[j][:],
-                    in_=sq_sum[:],
-                    func=ACT.Abs_reciprocal_sqrt,
-                    bias=EPS_LN,
-                    scale=1.0 / D,
-                )
-
-        def normalise_and_store(i):
-            for j in (2 * i, 2 * i + 1):
-                result = work.tile([P, D], F32, name="result")
-                nc.vector.tensor_scalar(
-                    out=result[:],
-                    in0=summed[j][:],
-                    scalar1=neg_mean2[j][:, 0:1],
-                    scalar2=rstd2[j][:, 0:1],
-                    op0=ALU.add,
-                    op1=ALU.mult,
-                )
-                nc.sync.dma_start(out=out_rows[:, j, :], in_=result[:])
-
-        transposes(0)
-        quantise(0)
+            load_xy(2 * i + 1)
+        load_x(TILES // 2 - 1)
 
         scale_rows = psum_acc.tile([P, D], F32, name="acc")
         nc.tensor.matmul(scale_rows[:], lhsT=ones[:], rhs=vectors[:, 0:D], start=True, stop=True)
@@ -256,16 +110,160 @@ def tile_bdhlayer_pc_kernel(
         gain = keep.tile([P, D], F32)
         nc.vector.tensor_tensor(out=gain[:], in0=regulation[:], in1=scale_rows[:], op=ALU.mult)
 
-        for i in range(PAIRS):
-            multiply(i)
-            if i + 1 < PAIRS:
-                transposes(i + 1)
-            first_stats(i)
-            if i > 0:
-                normalise_and_store(i - 1)
-            centre_and_gain(i)
-            if i + 1 < PAIRS:
-                quantise(i + 1)
-            add_tokens(i)
-            second_stats(i)
-        normalise_and_store(PAIRS - 1)
+        banks = {}
+        grouped = {}
+        codes = {}
+        planes = {}
+        acc = {}
+        stats = {}
+        mean_var = {}
+        rstd1 = {}
+        centred = {}
+        summed = {}
+        z_sum = {}
+        neg_mean2 = {}
+        rstd2 = {}
+
+        def transposes(j):
+            words = xs[j][:].bitcast(F32)
+            for first, count in BANK_SPLIT:
+                xt = psum_t.tile([P, count, 2, P], F32, name="xt%d" % count)
+                banks[(j, first)] = xt
+                for s in range(count):
+                    g = first + s
+                    for u in range(2):
+                        nc.tensor.transpose(
+                            xt[:, s, u, :],
+                            words[:, WORDS * g + u : WORDS * (g + 1) : 2],
+                            ident[:],
+                        )
+
+        def copy_out(j):
+            grouped[j] = stage.tile([P, PASSES * K_PASS], BF16, align_bytes=64, name="grouped")
+            for first, count in BANK_SPLIT:
+                nc.scalar.copy(
+                    out=grouped[j][:]
+                    .bitcast(F32)[:, WORDS * first : WORDS * (first + count)]
+                    .rearrange("p (s r u) -> p s r u", s=count, u=2),
+                    in_=banks[(j, first)][:].rearrange("p s u r -> p s r u"),
+                )
+
+        def quantise(j):
+            codes[j] = stage.tile([P, PASSES * P], U32, align_bytes=64, name="codes")
+            planes[j] = stage.tile([P, PASSES * P], U8, align_bytes=64, name="planes")
+            for first, count in BANK_SPLIT:
+                nc.vector.quantize_mx(
+                    out=codes[j][:, P * first : P * (first + count)].bitcast(FP8X4),
+                    scales=planes[j][:, P * first : P * (first + count)],
+                    in_=grouped[j][:, K_PASS * first : K_PASS * (first + count)],
+                )
+
+        def multiply(j):
+            acc[j] = psum_acc.tile([P, D], F32, name="acc")
+            for g in range(PASSES):
+                nc.tensor.matmul_mx(
+                    out=acc[j][:],
+                    lhsT=codes[j][:, P * g : P * (g + 1)].bitcast(FP8X4),
+                    lhsT_scale=planes[j][:, P * g : P * (g + 1)],
+                    rhs=w_words[:, g, :].bitcast(FP4X4),
+                    rhs_scale=w_planes[:, g, :],
+                    start=(g == 0),
+                    stop=(g == PASSES - 1),
+                )
+
+        def first_stats(j):
+            stats[j] = small.tile([P, 6], F32, name="stats")
+            nc.vector.bn_stats(out=stats[j][:], in_=acc[j][:])
+
+        def first_mean_rstd(j):
+            mean_var[j] = small.tile([P, 2], F32, name="mean_var")
+            nc.vector.bn_aggr(out=mean_var[j][:], in_=stats[j][:])
+            rstd1[j] = small.tile([P, 1], F32, name="rstd1")
+            nc.scalar.activation(
+                out=rstd1[j][:],
+                in_=mean_var[j][:, 1:2],
+                func=ACT.Abs_reciprocal_sqrt,
+                bias=EPS_LN,
+                scale=1.0,
+            )
+
+        def centre_and_gain(j):
+            centred[j] = work.tile([P, D], F32, name="centred")
+            nc.vector.scalar_tensor_tensor(
+                out=centred[j][:],
+                in0=acc[j][:],
+                scalar=mean_var[j][:, 0:1],
+                in1=gain[:],
+                op0=ALU.subtract,
+                op1=ALU.mult,
+            )
+
+        def add_tokens(j):
+            summed[j] = work.tile([P, D], F32, name="summed")
+            z_sum[j] = small.tile([P, 1], F32, name="z_sum")
+            nc.vector.scalar_tensor_tensor(
+                out=summed[j][:],
+                in0=centred[j][:],
+                scalar=rstd1[j][:, 0:1],
+                in1=x_in[j // 2][:, j % 2, :],
+                op0=ALU.mult,
+                op1=ALU.add,
+                accum_out=z_sum[j][:],
+            )
+            neg_mean2[j] = small.tile([P, 1], F32, name="neg_mean2")
+            nc.scalar.mul(out=neg_mean2[j][:], in_=z_sum[j][:], mul=-1.0 / D)
+
+        def second_rstd(j):
+            squares = work.tile([P, D], BF16, name="squares")
+            sq_sum = small.tile([P, 1], F32, name="sq_sum")
+            nc.scalar.activation(
+                out=squares[:],
+                in_=summed[j][:],
+                func=ACT.Square,
+                bias=neg_mean2[j][:, 0:1],
+                scale=1.0,
+                accum_out=sq_sum[:],
+            )
+            rstd2[j] = small.tile([P, 1], F32, name="rstd2")
+            nc.scalar.activation(
+                out=rstd2[j][:],
+                in_=sq_sum[:],
+                func=ACT.Abs_reciprocal_sqrt,
+                bias=EPS_LN,
+                scale=1.0 / D,
+            )
+
+        def normalise_and_store(j):
+            result = work.tile([P, D], F32, name="result")
+            nc.gpsimd.tensor_scalar(
+                out=result[:],
+                in0=summed[j][:],
+                scalar1=neg_mean2[j][:, 0:1],
+                scalar2=rstd2[j][:, 0:1],
+                op0=ALU.add,
+                op1=ALU.mult,
+            )
+            nc.sync.dma_start(out=out_rows[:, j, :], in_=result[:])
+
+        def live(j):
+            return 0 <= j < TILES
+
+        for j in range(-4, TILES + 1):
+            if live(j - 1):
+                add_tokens(j - 1)
+            if live(j):
+                first_mean_rstd(j)
+            if live(j - 1):
+                second_rstd(j - 1)
+                normalise_and_store(j - 1)
+            if live(j + 2):
+                quantise(j + 2)
+                multiply(j + 2)
+            if live(j + 4):
+                transposes(j + 4)
+            if live(j + 3):
+                copy_out(j + 3)
+            if live(j):
+                centre_and_gain(j)
+            if live(j + 1):
+                first_stats(j + 1)

@@ -121,7 +121,7 @@ def tile_bdhlayer_pc_kernel(
         centred = {}
         summed = {}
         z_sum = {}
-        neg_mean2 = {}
+        sq_sum = {}
         rstd2 = {}
 
         def transposes(j):
@@ -210,35 +210,37 @@ def tile_bdhlayer_pc_kernel(
                 op1=ALU.add,
                 accum_out=z_sum[j][:],
             )
-            neg_mean2[j] = small.tile([P, 1], F32, name="neg_mean2")
-            nc.scalar.mul(out=neg_mean2[j][:], in_=z_sum[j][:], mul=-1.0 / D)
 
-        def second_rstd(j):
+        def sum_squares(j):
             squares = work.tile([P, D], BF16, name="squares")
-            sq_sum = small.tile([P, 1], F32, name="sq_sum")
+            sq_sum[j] = small.tile([P, 1], F32, name="sq_sum")
             nc.scalar.activation(
                 out=squares[:],
                 in_=summed[j][:],
                 func=ACT.Square,
-                bias=neg_mean2[j][:, 0:1],
-                scale=1.0,
-                accum_out=sq_sum[:],
+                bias=z_sum[j][:, 0:1],
+                scale=-1.0 * D,
+                accum_out=sq_sum[j][:],
             )
+
+        def second_rstd(j):
             rstd2[j] = small.tile([P, 1], F32, name="rstd2")
             nc.scalar.activation(
                 out=rstd2[j][:],
-                in_=sq_sum[:],
+                in_=sq_sum[j][:],
                 func=ACT.Abs_reciprocal_sqrt,
                 bias=EPS_LN,
-                scale=1.0 / D,
+                scale=1.0 / (D * D * D),
             )
 
         def normalise_and_store(j):
+            neg_mean2 = small.tile([P, 1], F32, name="neg_mean2")
+            nc.vector.tensor_scalar_mul(out=neg_mean2[:], in0=z_sum[j][:], scalar1=-1.0 / D)
             result = work.tile([P, D], F32, name="result")
             nc.gpsimd.tensor_scalar(
                 out=result[:],
                 in0=summed[j][:],
-                scalar1=neg_mean2[j][:, 0:1],
+                scalar1=neg_mean2[:, 0:1],
                 scalar2=rstd2[j][:, 0:1],
                 op0=ALU.add,
                 op1=ALU.mult,
@@ -248,14 +250,20 @@ def tile_bdhlayer_pc_kernel(
         def live(j):
             return 0 <= j < TILES
 
-        for j in range(-4, TILES + 1):
+        for j in range(-4, TILES + 2):
             if live(j - 1):
                 add_tokens(j - 1)
+                sum_squares(j - 1)
             if live(j):
                 first_mean_rstd(j)
             if live(j - 1):
                 second_rstd(j - 1)
-                normalise_and_store(j - 1)
+            if live(j - 2):
+                normalise_and_store(j - 2)
+            if live(j):
+                centre_and_gain(j)
+            if live(j + 1):
+                first_stats(j + 1)
             if live(j + 2):
                 quantise(j + 2)
                 multiply(j + 2)
@@ -263,7 +271,3 @@ def tile_bdhlayer_pc_kernel(
                 transposes(j + 4)
             if live(j + 3):
                 copy_out(j + 3)
-            if live(j):
-                centre_and_gain(j)
-            if live(j + 1):
-                first_stats(j + 1)

@@ -46,18 +46,16 @@ def tile_bdhlayer_pc_kernel(
         psum_acc = ctx.enter_context(tc.psum_pool(name="psum_acc", bufs=3))
         ctx.enter_context(tc.manual_schedule())
 
-        vectors = keep.tile([P, 2 * D], BF16)
-        nc.vector.memset(vectors[:], 0.0)
         w_planes = keep.tile([P, PASSES, D], U8, align_bytes=64)
         nc.vector.memset(w_planes[:].bitcast(I32), 0)
+        padded = keep.tile([P, 2 * D], BF16)
+        nc.vector.memset(padded[:], 0.0)
         ones = keep.tile([P, P], BF16)
         nc.vector.memset(ones[:], 1.0)
         ident = keep.tile([P, P], F32)
         make_identity(nc, ident[:])
 
-        nc.scalar.dma_start(out=vectors[0:1, 0:D], in_=scale.unsqueeze(0))
-        nc.scalar.dma_start(out=vectors[0:1, D : 2 * D], in_=running_activity.unsqueeze(0))
-
+        vectors = keep.tile([1, 2 * D], BF16)
         xs = []
         for j in range(TILES):
             xs.append(keep.tile([P, HEADS * HEAD_DIM], BF16, name="xs%d" % j))
@@ -74,6 +72,8 @@ def tile_bdhlayer_pc_kernel(
         def load_x(i):
             nc.sync.dma_start(out=x_in[i][:], in_=x_rows[:, 2 * i : 2 * i + 2, :])
 
+        nc.sync.dma_start(out=vectors[0:1, 0:D], in_=scale.unsqueeze(0))
+        nc.sync.dma_start(out=vectors[0:1, D : 2 * D], in_=running_activity.unsqueeze(0))
         load_xy(0)
         load_xy(1)
         for q in range(4):
@@ -93,11 +93,12 @@ def tile_bdhlayer_pc_kernel(
             load_xy(2 * i + 1)
         load_x(TILES // 2 - 1)
 
+        nc.vector.tensor_copy(out=padded[0:1, :], in_=vectors[0:1, :])
         scale_rows = psum_acc.tile([P, D], F32, name="acc")
-        nc.tensor.matmul(scale_rows[:], lhsT=ones[:], rhs=vectors[:, 0:D], start=True, stop=True)
+        nc.tensor.matmul(scale_rows[:], lhsT=ones[:], rhs=padded[:, 0:D], start=True, stop=True)
         activity_rows = psum_acc.tile([P, D], F32, name="acc")
         nc.tensor.matmul(
-            activity_rows[:], lhsT=ones[:], rhs=vectors[:, D : 2 * D], start=True, stop=True
+            activity_rows[:], lhsT=ones[:], rhs=padded[:, D : 2 * D], start=True, stop=True
         )
         regulation = keep.tile([P, D], F32)
         nc.scalar.activation(
@@ -258,12 +259,6 @@ def tile_bdhlayer_pc_kernel(
                 first_mean_rstd(j)
             if live(j - 1):
                 second_rstd(j - 1)
-            if live(j - 2):
-                normalise_and_store(j - 2)
-            if live(j):
-                centre_and_gain(j)
-            if live(j + 1):
-                first_stats(j + 1)
             if live(j + 2):
                 quantise(j + 2)
                 multiply(j + 2)
@@ -271,3 +266,9 @@ def tile_bdhlayer_pc_kernel(
                 transposes(j + 4)
             if live(j + 3):
                 copy_out(j + 3)
+            if live(j - 2):
+                normalise_and_store(j - 2)
+            if live(j):
+                centre_and_gain(j)
+            if live(j + 1):
+                first_stats(j + 1)

@@ -21,10 +21,23 @@ D = 512
 K_PASS = 512
 PASSES = HEADS * HEAD_DIM // K_PASS
 TILES = TOKENS // P
-WORDS = K_PASS // 2
+PAIR_WORDS = K_PASS // 2
 BANK_SPLIT = ((0, 2), (2, 1))
+QUADRANTS = 4
+SCALE_ROWS = 4
+BN_STATS_DIM = 6
+BN_AGGR_DIM = 2
 EPS_LN = 1e-5
 TARGET_ACTIVITY = 0.1
+EPS_ACTIVITY = 1e-6
+
+TRANSPOSE_AHEAD = 4
+COPY_AHEAD = 3
+QUANTISE_AHEAD = 2
+STATS_AHEAD = 1
+ADD_BEHIND = 1
+NORMALISE_BEHIND = 2
+VECTOR_FINISHES = 2
 
 FLOPS = 2 * TOKENS * HEADS * HEAD_DIM * D
 
@@ -76,12 +89,12 @@ def tile_bdhlayer_pc_kernel(
         nc.sync.dma_start(out=vectors[0:1, D : 2 * D], in_=running_activity.unsqueeze(0))
         load_xy(0)
         load_xy(1)
-        for q in range(4):
+        for q in range(QUADRANTS):
             nc.sync.dma_start(
-                out=w_planes[32 * q : 32 * q + 4].bitcast(I32),
-                in_=decoder_scales.bitcast(I32)[:, 4 * q : 4 * q + 4, :].rearrange(
-                    "g r w -> r g w"
-                ),
+                out=w_planes[32 * q : 32 * q + SCALE_ROWS].bitcast(I32),
+                in_=decoder_scales.bitcast(I32)[
+                    :, SCALE_ROWS * q : SCALE_ROWS * (q + 1), :
+                ].rearrange("g r w -> r g w"),
             )
         nc.sync.dma_start(
             out=w_words[:].bitcast(I32),
@@ -105,7 +118,7 @@ def tile_bdhlayer_pc_kernel(
             out=regulation[:],
             in_=activity_rows[:],
             func=ACT.Abs_reciprocal_sqrt,
-            bias=1e-6 / TARGET_ACTIVITY,
+            bias=EPS_ACTIVITY / TARGET_ACTIVITY,
             scale=1.0 / TARGET_ACTIVITY,
         )
         gain = keep.tile([P, D], F32)
@@ -135,7 +148,7 @@ def tile_bdhlayer_pc_kernel(
                     for u in range(2):
                         nc.tensor.transpose(
                             xt[:, s, u, :],
-                            words[:, WORDS * g + u : WORDS * (g + 1) : 2],
+                            words[:, PAIR_WORDS * g + u : PAIR_WORDS * (g + 1) : 2],
                             ident[:],
                         )
 
@@ -144,7 +157,7 @@ def tile_bdhlayer_pc_kernel(
             for first, count in BANK_SPLIT:
                 nc.scalar.copy(
                     out=grouped[j][:]
-                    .bitcast(F32)[:, WORDS * first : WORDS * (first + count)]
+                    .bitcast(F32)[:, PAIR_WORDS * first : PAIR_WORDS * (first + count)]
                     .rearrange("p (s r u) -> p s r u", s=count, u=2),
                     in_=banks[(j, first)][:].rearrange("p s u r -> p s r u"),
                 )
@@ -173,11 +186,11 @@ def tile_bdhlayer_pc_kernel(
                 )
 
         def first_stats(j):
-            stats[j] = small.tile([P, 6], F32, name="stats")
+            stats[j] = small.tile([P, BN_STATS_DIM], F32, name="stats")
             nc.vector.bn_stats(out=stats[j][:], in_=acc[j][:])
 
         def first_mean_rstd(j):
-            mean_var[j] = small.tile([P, 2], F32, name="mean_var")
+            mean_var[j] = small.tile([P, BN_AGGR_DIM], F32, name="mean_var")
             nc.vector.bn_aggr(out=mean_var[j][:], in_=stats[j][:])
             rstd1[j] = small.tile([P, 1], F32, name="rstd1")
             nc.scalar.activation(
@@ -238,7 +251,8 @@ def tile_bdhlayer_pc_kernel(
             neg_mean2 = small.tile([P, 1], F32, name="neg_mean2")
             nc.vector.tensor_scalar_mul(out=neg_mean2[:], in0=z_sum[j][:], scalar1=-1.0 / D)
             result = work.tile([P, D], F32, name="result")
-            nc.gpsimd.tensor_scalar(
+            engine = nc.vector if j >= TILES - VECTOR_FINISHES else nc.gpsimd
+            engine.tensor_scalar(
                 out=result[:],
                 in0=summed[j][:],
                 scalar1=neg_mean2[:, 0:1],
@@ -251,24 +265,24 @@ def tile_bdhlayer_pc_kernel(
         def live(j):
             return 0 <= j < TILES
 
-        for j in range(-4, TILES + 2):
-            if live(j - 1):
-                add_tokens(j - 1)
-                sum_squares(j - 1)
+        for j in range(-TRANSPOSE_AHEAD, TILES + NORMALISE_BEHIND):
+            if live(j - ADD_BEHIND):
+                add_tokens(j - ADD_BEHIND)
+                sum_squares(j - ADD_BEHIND)
             if live(j):
                 first_mean_rstd(j)
-            if live(j - 1):
-                second_rstd(j - 1)
-            if live(j + 2):
-                quantise(j + 2)
-                multiply(j + 2)
-            if live(j + 4):
-                transposes(j + 4)
-            if live(j + 3):
-                copy_out(j + 3)
-            if live(j - 2):
-                normalise_and_store(j - 2)
+            if live(j - ADD_BEHIND):
+                second_rstd(j - ADD_BEHIND)
+            if live(j + QUANTISE_AHEAD):
+                quantise(j + QUANTISE_AHEAD)
+                multiply(j + QUANTISE_AHEAD)
+            if live(j + TRANSPOSE_AHEAD):
+                transposes(j + TRANSPOSE_AHEAD)
+            if live(j + COPY_AHEAD):
+                copy_out(j + COPY_AHEAD)
+            if live(j - NORMALISE_BEHIND):
+                normalise_and_store(j - NORMALISE_BEHIND)
             if live(j):
                 centre_and_gain(j)
-            if live(j + 1):
-                first_stats(j + 1)
+            if live(j + STATS_AHEAD):
+                first_stats(j + STATS_AHEAD)

@@ -38,6 +38,7 @@ STATS_AHEAD = 1
 ADD_BEHIND = 1
 NORMALISE_BEHIND = 2
 VECTOR_FINISHES = 2
+SCALAR_FINISHES = 2
 
 FLOPS = 2 * TOKENS * HEADS * HEAD_DIM * D
 
@@ -262,16 +263,38 @@ def tile_bdhlayer_pc_kernel(
             )
             nc.sync.dma_start(out=out_rows[:, j, :], in_=result[:])
 
+        def scalar_normalise_and_store(j):
+            neg_mean2 = small.tile([P, 1], F32, name="neg_mean2")
+            nc.scalar.activation(
+                out=neg_mean2[:], in_=z_sum[j][:], func=ACT.Copy, scale=-1.0 / D
+            )
+            shift = small.tile([P, 1], F32, name="shift")
+            nc.scalar.activation(
+                out=shift[:], in_=neg_mean2[:], func=ACT.Copy, scale=rstd2[j][:, 0:1]
+            )
+            result = work.tile([P, D], F32, name="result")
+            nc.scalar.activation(
+                out=result[:],
+                in_=summed[j][:],
+                func=ACT.Identity,
+                bias=shift[:, 0:1],
+                scale=rstd2[j][:, 0:1],
+            )
+            nc.sync.dma_start(out=out_rows[:, j, :], in_=result[:])
+
+        def by_scalar(j):
+            return TILES - VECTOR_FINISHES - SCALAR_FINISHES <= j < TILES - VECTOR_FINISHES
+
         def live(j):
             return 0 <= j < TILES
 
         for j in range(-TRANSPOSE_AHEAD, TILES + NORMALISE_BEHIND):
             if live(j - ADD_BEHIND):
                 add_tokens(j - ADD_BEHIND)
-                sum_squares(j - ADD_BEHIND)
             if live(j):
                 first_mean_rstd(j)
             if live(j - ADD_BEHIND):
+                sum_squares(j - ADD_BEHIND)
                 second_rstd(j - ADD_BEHIND)
             if live(j + QUANTISE_AHEAD):
                 quantise(j + QUANTISE_AHEAD)
@@ -280,8 +303,10 @@ def tile_bdhlayer_pc_kernel(
                 transposes(j + TRANSPOSE_AHEAD)
             if live(j + COPY_AHEAD):
                 copy_out(j + COPY_AHEAD)
-            if live(j - NORMALISE_BEHIND):
+            if live(j - NORMALISE_BEHIND) and not by_scalar(j - NORMALISE_BEHIND):
                 normalise_and_store(j - NORMALISE_BEHIND)
+            if by_scalar(j - ADD_BEHIND):
+                scalar_normalise_and_store(j - ADD_BEHIND)
             if live(j):
                 centre_and_gain(j)
             if live(j + STATS_AHEAD):

@@ -38,6 +38,8 @@ STATS_AHEAD = 1
 ADD_BEHIND = 1
 NORMALISE_BEHIND = 2
 VECTOR_FINISHES = 2
+CLOCK_RAISERS_FIRST = 12
+CLOCK_RAISERS_LATER = 4
 SCALAR_FINISHES = 2
 
 FLOPS = 2 * TOKENS * HEADS * HEAD_DIM * D
@@ -58,6 +60,7 @@ def tile_bdhlayer_pc_kernel(
         small = ctx.enter_context(tc.tile_pool(name="small", bufs=4))
         psum_t = ctx.enter_context(tc.psum_pool(name="psum_t", bufs=2))
         psum_acc = ctx.enter_context(tc.psum_pool(name="psum_acc", bufs=3))
+        psum_idle = ctx.enter_context(tc.psum_pool(name="psum_idle", bufs=1))
         ctx.enter_context(tc.manual_schedule())
 
         w_planes = keep.tile([P, PASSES, D], U8, align_bytes=64)
@@ -66,6 +69,15 @@ def tile_bdhlayer_pc_kernel(
         nc.vector.memset(padded[:], 0.0)
         ones = keep.tile([P, P], BF16)
         nc.vector.memset(ones[:], 1.0)
+        ident_bf = keep.tile([P, P], BF16)
+        make_identity(nc, ident_bf[:])
+        unread = psum_idle.tile([P, P], F32, name="unread")
+
+        def raise_clock(times):
+            for i in range(times):
+                nc.tensor.matmul(unread[:], lhsT=ident_bf[:], rhs=ident_bf[:], start=True, stop=True)
+
+        raise_clock(CLOCK_RAISERS_FIRST)
         ident = keep.tile([P, P], F32)
         make_identity(nc, ident[:])
 
@@ -301,6 +313,8 @@ def tile_bdhlayer_pc_kernel(
                 multiply(j + QUANTISE_AHEAD)
             if live(j + TRANSPOSE_AHEAD):
                 transposes(j + TRANSPOSE_AHEAD)
+            if 0 <= j + TRANSPOSE_AHEAD < 2:
+                raise_clock(CLOCK_RAISERS_LATER)
             if live(j + COPY_AHEAD):
                 copy_out(j + COPY_AHEAD)
             if live(j - NORMALISE_BEHIND) and not by_scalar(j - NORMALISE_BEHIND):

@@ -38,7 +38,7 @@ STATS_AHEAD = 1
 ADD_BEHIND = 1
 NORMALISE_BEHIND = 2
 VECTOR_FINISHES = 2
-CLOCK_RAISERS_FIRST = 12
+CLOCK_RAISERS_FIRST = 20
 CLOCK_RAISERS_LATER = 4
 SCALAR_FINISHES = 2
 
@@ -69,13 +69,13 @@ def tile_bdhlayer_pc_kernel(
         nc.vector.memset(padded[:], 0.0)
         ones = keep.tile([P, P], BF16)
         nc.vector.memset(ones[:], 1.0)
-        ident_bf = keep.tile([P, P], BF16)
-        make_identity(nc, ident_bf[:])
+        zeros = keep.tile([P, P], BF16)
+        nc.gpsimd.memset(zeros[:], 0.0)
         unread = psum_idle.tile([P, P], F32, name="unread")
 
         def raise_clock(times):
             for i in range(times):
-                nc.tensor.matmul(unread[:], lhsT=ident_bf[:], rhs=ident_bf[:], start=True, stop=True)
+                nc.tensor.matmul(unread[:], lhsT=zeros[:], rhs=zeros[:], start=True, stop=True)
 
         raise_clock(CLOCK_RAISERS_FIRST)
         ident = keep.tile([P, P], F32)

@@ -63,6 +63,11 @@ def tile_bdhlayer_pc_kernel(
         psum_idle = ctx.enter_context(tc.psum_pool(name="psum_idle", bufs=1))
         ctx.enter_context(tc.manual_schedule())
 
+        one = keep.tile([P, 1], F32)
+        nc.gpsimd.memset(one[:], 1.0)
+        unused_rsqrt = keep.tile([P, 1], F32)
+        nc.scalar.activation(out=unused_rsqrt[:], in_=one[:], func=ACT.Abs_reciprocal_sqrt)
+
         w_planes = keep.tile([P, PASSES, D], U8, align_bytes=64)
         nc.vector.memset(w_planes[:].bitcast(I32), 0)
         padded = keep.tile([P, 2 * D], BF16)
@@ -90,9 +95,12 @@ def tile_bdhlayer_pc_kernel(
             x_in.append(keep.tile([P, 2, D], BF16, name="x_in%d" % i))
         w_words = keep.tile([P, PASSES, 2 * D], U8, align_bytes=64)
 
-        def load_xy(j):
+        def load_xy(j, first_head=0, heads=HEADS):
             nc.sync.dma_start(
-                out=xs[j][:].rearrange("p (h n) -> p h n", h=HEADS), in_=xy_tiles[j]
+                out=xs[j][:].rearrange("p (h n) -> p h n", h=HEADS)[
+                    :, first_head : first_head + heads, :
+                ],
+                in_=xy_tiles[j][:, first_head : first_head + heads, :],
             )
 
         def load_x(i):
@@ -100,7 +108,8 @@ def tile_bdhlayer_pc_kernel(
 
         nc.sync.dma_start(out=vectors[0:1, 0:D], in_=scale.unsqueeze(0))
         nc.sync.dma_start(out=vectors[0:1, D : 2 * D], in_=running_activity.unsqueeze(0))
-        load_xy(0)
+        for first, count in BANK_SPLIT:
+            load_xy(0, HEADS // PASSES * first, HEADS // PASSES * count)
         load_xy(1)
         for q in range(QUADRANTS):
             nc.sync.dma_start(
@@ -120,22 +129,33 @@ def tile_bdhlayer_pc_kernel(
         load_x(TILES // 2 - 1)
 
         nc.vector.tensor_copy(out=padded[0:1, :], in_=vectors[0:1, :])
-        scale_rows = psum_acc.tile([P, D], F32, name="acc")
-        nc.tensor.matmul(scale_rows[:], lhsT=ones[:], rhs=padded[:, 0:D], start=True, stop=True)
-        activity_rows = psum_acc.tile([P, D], F32, name="acc")
-        nc.tensor.matmul(
-            activity_rows[:], lhsT=ones[:], rhs=padded[:, D : 2 * D], start=True, stop=True
-        )
         regulation = keep.tile([P, D], F32)
-        nc.scalar.activation(
-            out=regulation[:],
-            in_=activity_rows[:],
-            func=ACT.Abs_reciprocal_sqrt,
-            bias=EPS_ACTIVITY / TARGET_ACTIVITY,
-            scale=1.0 / TARGET_ACTIVITY,
-        )
         gain = keep.tile([P, D], F32)
-        nc.vector.tensor_tensor(out=gain[:], in0=regulation[:], in1=scale_rows[:], op=ALU.mult)
+        spread = {}
+
+        def spread_vectors():
+            spread["scale"] = psum_acc.tile([P, D], F32, name="acc")
+            nc.tensor.matmul(
+                spread["scale"][:], lhsT=ones[:], rhs=padded[:, 0:D], start=True, stop=True
+            )
+            spread["activity"] = psum_acc.tile([P, D], F32, name="acc")
+            nc.tensor.matmul(
+                spread["activity"][:], lhsT=ones[:], rhs=padded[:, D : 2 * D], start=True, stop=True
+            )
+
+        def regulate():
+            nc.scalar.activation(
+                out=regulation[:],
+                in_=spread["activity"][:],
+                func=ACT.Abs_reciprocal_sqrt,
+                bias=EPS_ACTIVITY / TARGET_ACTIVITY,
+                scale=1.0 / TARGET_ACTIVITY,
+            )
+
+        def build_gain():
+            nc.vector.tensor_tensor(
+                out=gain[:], in0=regulation[:], in1=spread["scale"][:], op=ALU.mult
+            )
 
         banks = {}
         grouped = {}
@@ -164,6 +184,8 @@ def tile_bdhlayer_pc_kernel(
                             words[:, PAIR_WORDS * g + u : PAIR_WORDS * (g + 1) : 2],
                             ident[:],
                         )
+                if j == 0 and first == 0:
+                    spread_vectors()
 
         def copy_out(j):
             grouped[j] = stage.tile([P, PASSES * K_PASS], BF16, align_bytes=64, name="grouped")
@@ -317,6 +339,10 @@ def tile_bdhlayer_pc_kernel(
                 raise_clock(CLOCK_RAISERS_LATER)
             if live(j + COPY_AHEAD):
                 copy_out(j + COPY_AHEAD)
+            if j + COPY_AHEAD == 0:
+                regulate()
+            if j + QUANTISE_AHEAD == 0:
+                build_gain()
             if live(j - NORMALISE_BEHIND) and not by_scalar(j - NORMALISE_BEHIND):
                 normalise_and_store(j - NORMALISE_BEHIND)
             if by_scalar(j - ADD_BEHIND):

@@ -37,10 +37,11 @@ QUANTISE_AHEAD = 2
 STATS_AHEAD = 1
 ADD_BEHIND = 1
 NORMALISE_BEHIND = 2
-VECTOR_FINISHES = 2
 CLOCK_RAISERS_FIRST = 20
 CLOCK_RAISERS_LATER = 4
-SCALAR_FINISHES = 2
+SCALAR_E = ()
+VECTOR_E = (5, 6, 7,)
+SCALAR_STATS = (6,)
 
 FLOPS = 2 * TOKENS * HEADS * HEAD_DIM * D
 
@@ -55,7 +56,7 @@ def tile_bdhlayer_pc_kernel(
 
     with ExitStack() as ctx:
         keep = ctx.enter_context(tc.tile_pool(name="keep", bufs=1))
-        stage = ctx.enter_context(tc.tile_pool(name="stage", bufs=3))
+        stage = ctx.enter_context(tc.tile_pool(name="stage", bufs=4))
         work = ctx.enter_context(tc.tile_pool(name="work", bufs=4))
         small = ctx.enter_context(tc.tile_pool(name="small", bufs=4))
         psum_t = ctx.enter_context(tc.psum_pool(name="psum_t", bufs=2))
@@ -169,6 +170,8 @@ def tile_bdhlayer_pc_kernel(
         summed = {}
         z_sum = {}
         sq_sum = {}
+        sums1 = {}
+        neg_mean = {}
         rstd2 = {}
 
         def transposes(j):
@@ -197,10 +200,12 @@ def tile_bdhlayer_pc_kernel(
                     in_=banks[(j, first)][:].rearrange("p s u r -> p s r u"),
                 )
 
-        def quantise(j):
+        def new_codes(j):
             codes[j] = stage.tile([P, PASSES * P], U32, align_bytes=64, name="codes")
             planes[j] = stage.tile([P, PASSES * P], U8, align_bytes=64, name="planes")
-            for first, count in BANK_SPLIT:
+
+        def quantise_part(j, part):
+            for first, count in (BANK_SPLIT[part],):
                 nc.vector.quantize_mx(
                     out=codes[j][:, P * first : P * (first + count)].bitcast(FP8X4),
                     scales=planes[j][:, P * first : P * (first + count)],
@@ -220,20 +225,52 @@ def tile_bdhlayer_pc_kernel(
                     stop=(g == PASSES - 1),
                 )
 
+        def scalar_first_stats(j):
+            mean_var[j] = small.tile([P, BN_AGGR_DIM], F32, name="mean_var")
+            sums1[j] = small.tile([P, 1], F32, name="sq1")
+            dump = work.tile([P, D], BF16, name="squares")
+            nc.scalar.activation(
+                out=dump[:],
+                in_=acc[j][:],
+                func=ACT.Copy,
+                scale=1.0 / D,
+                accum_out=mean_var[j][:, 0:1],
+            )
+
+        def scalar_squares(j):
+            sq1 = sums1[j]
+            dump2 = work.tile([P, D], BF16, name="squares")
+            nc.scalar.activation(
+                out=dump2[:],
+                in_=acc[j][:],
+                func=ACT.Square,
+                bias=mean_var[j][:, 0:1],
+                scale=-1.0,
+                accum_out=sq1[:],
+            )
+
         def first_stats(j):
             stats[j] = small.tile([P, BN_STATS_DIM], F32, name="stats")
             nc.vector.bn_stats(out=stats[j][:], in_=acc[j][:])
 
-        def first_mean_rstd(j):
+        def aggregate(j):
+            if j in SCALAR_STATS:
+                return
             mean_var[j] = small.tile([P, BN_AGGR_DIM], F32, name="mean_var")
             nc.vector.bn_aggr(out=mean_var[j][:], in_=stats[j][:])
+
+        def first_rstd(j):
             rstd1[j] = small.tile([P, 1], F32, name="rstd1")
+            if j in SCALAR_STATS:
+                variance, factor = sums1[j][:], 1.0 / D
+            else:
+                variance, factor = mean_var[j][:, 1:2], 1.0
             nc.scalar.activation(
                 out=rstd1[j][:],
-                in_=mean_var[j][:, 1:2],
+                in_=variance,
                 func=ACT.Abs_reciprocal_sqrt,
                 bias=EPS_LN,
-                scale=1.0,
+                scale=factor,
             )
 
         def centre_and_gain(j):
@@ -282,15 +319,17 @@ def tile_bdhlayer_pc_kernel(
                 scale=1.0 / (D * D * D),
             )
 
-        def normalise_and_store(j):
-            neg_mean2 = small.tile([P, 1], F32, name="neg_mean2")
-            nc.vector.tensor_scalar_mul(out=neg_mean2[:], in0=z_sum[j][:], scalar1=-1.0 / D)
+        def negate_mean(j):
+            neg_mean[j] = small.tile([P, 1], F32, name="neg_mean")
+            nc.vector.tensor_scalar_mul(out=neg_mean[j][:], in0=z_sum[j][:], scalar1=-1.0 / D)
+
+        def normalise(j):
             result = work.tile([P, D], F32, name="result")
-            engine = nc.vector if j >= TILES - VECTOR_FINISHES else nc.gpsimd
+            engine = nc.vector if j in VECTOR_E else nc.gpsimd
             engine.tensor_scalar(
                 out=result[:],
                 in0=summed[j][:],
-                scalar1=neg_mean2[:, 0:1],
+                scalar1=neg_mean[j][:, 0:1],
                 scalar2=rstd2[j][:, 0:1],
                 op0=ALU.add,
                 op1=ALU.mult,
@@ -317,37 +356,72 @@ def tile_bdhlayer_pc_kernel(
             nc.sync.dma_start(out=out_rows[:, j, :], in_=result[:])
 
         def by_scalar(j):
-            return TILES - VECTOR_FINISHES - SCALAR_FINISHES <= j < TILES - VECTOR_FINISHES
+            return j in SCALAR_E
 
         def live(j):
             return 0 <= j < TILES
 
-        for j in range(-TRANSPOSE_AHEAD, TILES + NORMALISE_BEHIND):
-            if live(j - ADD_BEHIND):
-                add_tokens(j - ADD_BEHIND)
+        for j in range(-4, 6):
+            if j + 1 in SCALAR_STATS:
+                scalar_first_stats(j + 1)
+            if j + 1 in SCALAR_STATS:
+                scalar_squares(j + 1)
+            if live(j - 1):
+                add_tokens(j - 1)
             if live(j):
-                first_mean_rstd(j)
-            if live(j - ADD_BEHIND):
-                sum_squares(j - ADD_BEHIND)
-                second_rstd(j - ADD_BEHIND)
-            if live(j + QUANTISE_AHEAD):
-                quantise(j + QUANTISE_AHEAD)
-                multiply(j + QUANTISE_AHEAD)
-            if live(j + TRANSPOSE_AHEAD):
-                transposes(j + TRANSPOSE_AHEAD)
-            if 0 <= j + TRANSPOSE_AHEAD < 2:
+                aggregate(j)
+            if live(j):
+                first_rstd(j)
+            if live(j - 1):
+                sum_squares(j - 1)
+            if live(j - 1):
+                second_rstd(j - 1)
+            if live(j + 2):
+                new_codes(j + 2)
+                quantise_part(j + 2, 0)
+            if live(j + 2):
+                quantise_part(j + 2, 1)
+            if live(j + 2):
+                multiply(j + 2)
+            if live(j + 4):
+                transposes(j + 4)
+            if j + 4 in (0, 1,):
                 raise_clock(CLOCK_RAISERS_LATER)
-            if live(j + COPY_AHEAD):
-                copy_out(j + COPY_AHEAD)
-            if j + COPY_AHEAD == 0:
+            if live(j + 3):
+                copy_out(j + 3)
+            if j + 3 == 0:
                 regulate()
-            if j + QUANTISE_AHEAD == 0:
+            if j + 2 == 0:
                 build_gain()
-            if live(j - NORMALISE_BEHIND) and not by_scalar(j - NORMALISE_BEHIND):
-                normalise_and_store(j - NORMALISE_BEHIND)
-            if by_scalar(j - ADD_BEHIND):
-                scalar_normalise_and_store(j - ADD_BEHIND)
+            if live(j - 2) and not by_scalar(j - 2):
+                negate_mean(j - 2)
+                normalise(j - 2)
+            if by_scalar(j - 1):
+                scalar_normalise_and_store(j - 1)
             if live(j):
                 centre_and_gain(j)
-            if live(j + STATS_AHEAD):
-                first_stats(j + STATS_AHEAD)
+            if live(j + 1) and j + 1 not in SCALAR_STATS:
+                first_stats(j + 1)
+        negate_mean(4)
+        normalise(4)
+        centre_and_gain(6)
+        first_stats(7)
+        add_tokens(5)
+        first_rstd(6)
+        sum_squares(5)
+        second_rstd(5)
+        aggregate(7)
+        first_rstd(7)
+        add_tokens(6)
+        sum_squares(6)
+        negate_mean(5)
+        centre_and_gain(7)
+        second_rstd(6)
+        normalise(5)
+        add_tokens(7)
+        sum_squares(7)
+        second_rstd(7)
+        negate_mean(6)
+        normalise(6)
+        negate_mean(7)
+        normalise(7)

@@ -39,11 +39,15 @@ ADD_BEHIND = 1
 NORMALISE_BEHIND = 2
 CLOCK_RAISERS_FIRST = 20
 CLOCK_RAISERS_LATER = 4
-SCALAR_E = ()
+SCALAR_E = (4,)
 VECTOR_E = (5, 6, 7,)
 SCALAR_STATS = (6,)
 
 FLOPS = 2 * TOKENS * HEADS * HEAD_DIM * D
+
+
+def splits(j):
+    return BANK_SPLIT
 
 
 def tile_bdhlayer_pc_kernel(
@@ -109,7 +113,7 @@ def tile_bdhlayer_pc_kernel(
 
         nc.sync.dma_start(out=vectors[0:1, 0:D], in_=scale.unsqueeze(0))
         nc.sync.dma_start(out=vectors[0:1, D : 2 * D], in_=running_activity.unsqueeze(0))
-        for first, count in BANK_SPLIT:
+        for first, count in splits(0):
             load_xy(0, HEADS // PASSES * first, HEADS // PASSES * count)
         load_xy(1)
         for q in range(QUADRANTS):
@@ -176,7 +180,7 @@ def tile_bdhlayer_pc_kernel(
 
         def transposes(j):
             words = xs[j][:].bitcast(F32)
-            for first, count in BANK_SPLIT:
+            for first, count in splits(j):
                 xt = psum_t.tile([P, count, 2, P], F32, name="xt%d" % count)
                 banks[(j, first)] = xt
                 for s in range(count):
@@ -192,7 +196,7 @@ def tile_bdhlayer_pc_kernel(
 
         def copy_out(j):
             grouped[j] = stage.tile([P, PASSES * K_PASS], BF16, align_bytes=64, name="grouped")
-            for first, count in BANK_SPLIT:
+            for first, count in splits(j):
                 nc.scalar.copy(
                     out=grouped[j][:]
                     .bitcast(F32)[:, PAIR_WORDS * first : PAIR_WORDS * (first + count)]
@@ -205,7 +209,7 @@ def tile_bdhlayer_pc_kernel(
             planes[j] = stage.tile([P, PASSES * P], U8, align_bytes=64, name="planes")
 
         def quantise_part(j, part):
-            for first, count in (BANK_SPLIT[part],):
+            for first, count in (splits(j)[part],):
                 nc.vector.quantize_mx(
                     out=codes[j][:, P * first : P * (first + count)].bitcast(FP8X4),
                     scales=planes[j][:, P * first : P * (first + count)],
@@ -402,8 +406,6 @@ def tile_bdhlayer_pc_kernel(
                 centre_and_gain(j)
             if live(j + 1) and j + 1 not in SCALAR_STATS:
                 first_stats(j + 1)
-        negate_mean(4)
-        normalise(4)
         centre_and_gain(6)
         first_stats(7)
         add_tokens(5)

@@ -191,8 +191,6 @@ def tile_bdhlayer_pc_kernel(
                             words[:, PAIR_WORDS * g + u : PAIR_WORDS * (g + 1) : 2],
                             ident[:],
                         )
-                if j == 0 and first == 0:
-                    spread_vectors()
 
         def copy_out(j):
             grouped[j] = stage.tile([P, PASSES * K_PASS], BF16, align_bytes=64, name="grouped")
@@ -365,7 +363,38 @@ def tile_bdhlayer_pc_kernel(
         def live(j):
             return 0 <= j < TILES
 
-        for j in range(-4, 6):
+        transposes(0)
+        spread_vectors()
+        raise_clock(4)
+        transposes(1)
+        raise_clock(4)
+        copy_out(0)
+        regulate()
+        new_codes(0)
+        for part in range(len(splits(0))):
+            quantise_part(0, part)
+        multiply(0)
+        transposes(2)
+        copy_out(1)
+        build_gain()
+        new_codes(1)
+        for part in range(len(splits(1))):
+            quantise_part(1, part)
+        multiply(1)
+        transposes(3)
+        copy_out(2)
+        first_stats(0)
+        aggregate(0)
+        first_rstd(0)
+        centre_and_gain(0)
+        new_codes(2)
+        for part in range(len(splits(2))):
+            quantise_part(2, part)
+        multiply(2)
+        transposes(4)
+        copy_out(3)
+        first_stats(1)
+        for j in range(1, 6):
             if j + 1 in SCALAR_STATS:
                 scalar_first_stats(j + 1)
             if j + 1 in SCALAR_STATS:
@@ -389,6 +418,8 @@ def tile_bdhlayer_pc_kernel(
                 multiply(j + 2)
             if live(j + 4):
                 transposes(j + 4)
+            if j + 4 == 0:
+                spread_vectors()
             if j + 4 in (0, 1,):
                 raise_clock(CLOCK_RAISERS_LATER)
             if live(j + 3):

@@ -39,7 +39,7 @@ ADD_BEHIND = 1
 NORMALISE_BEHIND = 2
 CLOCK_RAISERS_FIRST = 20
 CLOCK_RAISERS_LATER = 4
-SCALAR_E = (4,)
+SCALAR_E = ()
 VECTOR_E = (5, 6, 7,)
 SCALAR_STATS = (6,)
 
@@ -129,8 +129,8 @@ def tile_bdhlayer_pc_kernel(
         )
         for i in range(1, TILES // 2):
             load_xy(2 * i)
-            load_x(i - 1)
             load_xy(2 * i + 1)
+            load_x(i - 1)
         load_x(TILES // 2 - 1)
 
         nc.vector.tensor_copy(out=padded[0:1, :], in_=vectors[0:1, :])
@@ -176,6 +176,7 @@ def tile_bdhlayer_pc_kernel(
         sq_sum = {}
         sums1 = {}
         neg_mean = {}
+        shift_t = {}
         rstd2 = {}
 
         def transposes(j):
@@ -338,6 +339,39 @@ def tile_bdhlayer_pc_kernel(
             )
             nc.sync.dma_start(out=out_rows[:, j, :], in_=result[:])
 
+        def scalar_negate(j):
+            neg_mean[j] = small.tile([P, 1], F32, name="neg_mean_s")
+            nc.scalar.activation(out=neg_mean[j][:], in_=z_sum[j][:], func=ACT.Copy, scale=-1.0 / D)
+
+        def shift_of(j):
+            shift_t[j] = small.tile([P, 1], F32, name="shift_t")
+            nc.scalar.activation(
+                out=shift_t[j][:], in_=neg_mean[j][:], func=ACT.Copy, scale=rstd2[j][:, 0:1]
+            )
+
+        def pool_normalise(j):
+            result = work.tile([P, D], F32, name="result")
+            nc.gpsimd.tensor_scalar(
+                out=result[:],
+                in0=summed[j][:],
+                scalar1=rstd2[j][:, 0:1],
+                scalar2=shift_t[j][:, 0:1],
+                op0=ALU.mult,
+                op1=ALU.add,
+            )
+            nc.sync.dma_start(out=out_rows[:, j, :], in_=result[:])
+
+        def scalar_apply(j):
+            result = work.tile([P, D], F32, name="result")
+            nc.scalar.activation(
+                out=result[:],
+                in_=summed[j][:],
+                func=ACT.Identity,
+                bias=shift_t[j][:, 0:1],
+                scale=rstd2[j][:, 0:1],
+            )
+            nc.sync.dma_start(out=out_rows[:, j, :], in_=result[:])
+
         def scalar_normalise_and_store(j):
             neg_mean2 = small.tile([P, 1], F32, name="neg_mean2")
             nc.scalar.activation(
@@ -397,16 +431,22 @@ def tile_bdhlayer_pc_kernel(
         for j in range(1, 6):
             if j + 1 in SCALAR_STATS:
                 scalar_first_stats(j + 1)
-            if j + 1 in SCALAR_STATS:
-                scalar_squares(j + 1)
             if live(j - 1):
                 add_tokens(j - 1)
-            if live(j):
+            if live(j) and j not in SCALAR_STATS:
                 aggregate(j)
             if live(j):
                 first_rstd(j)
+            if live(j - 2):
+                shift_of(j - 2)
+            if j + 1 in SCALAR_STATS:
+                scalar_squares(j + 1)
             if live(j - 1):
                 sum_squares(j - 1)
+            if live(j + 3):
+                copy_out(j + 3)
+            if live(j - 1):
+                scalar_negate(j - 1)
             if live(j - 1):
                 second_rstd(j - 1)
             if live(j + 2):
@@ -418,43 +458,32 @@ def tile_bdhlayer_pc_kernel(
                 multiply(j + 2)
             if live(j + 4):
                 transposes(j + 4)
-            if j + 4 == 0:
-                spread_vectors()
-            if j + 4 in (0, 1,):
-                raise_clock(CLOCK_RAISERS_LATER)
-            if live(j + 3):
-                copy_out(j + 3)
-            if j + 3 == 0:
-                regulate()
-            if j + 2 == 0:
-                build_gain()
-            if live(j - 2) and not by_scalar(j - 2):
-                negate_mean(j - 2)
-                normalise(j - 2)
-            if by_scalar(j - 1):
-                scalar_normalise_and_store(j - 1)
+            if live(j - 2):
+                pool_normalise(j - 2)
             if live(j):
                 centre_and_gain(j)
             if live(j + 1) and j + 1 not in SCALAR_STATS:
                 first_stats(j + 1)
+        first_rstd(6)
+        shift_of(4)
         centre_and_gain(6)
         first_stats(7)
         add_tokens(5)
-        first_rstd(6)
+        scalar_apply(4)
         sum_squares(5)
+        scalar_negate(5)
         second_rstd(5)
         aggregate(7)
         first_rstd(7)
         add_tokens(6)
         sum_squares(6)
-        negate_mean(5)
+        scalar_negate(6)
         centre_and_gain(7)
         second_rstd(6)
-        normalise(5)
         add_tokens(7)
         sum_squares(7)
         second_rstd(7)
-        negate_mean(6)
-        normalise(6)
+        normalise(5)
         negate_mean(7)
+        normalise(6)
         normalise(7)

@@ -68,6 +68,9 @@ def tile_bdhlayer_pc_kernel(
         psum_idle = ctx.enter_context(tc.psum_pool(name="psum_idle", bufs=1))
         ctx.enter_context(tc.manual_schedule())
 
+        vectors = keep.tile([1, 2 * D], BF16)
+        nc.scalar.dma_start(out=vectors[0:1, 0:D], in_=scale.unsqueeze(0))
+        nc.scalar.dma_start(out=vectors[0:1, D : 2 * D], in_=running_activity.unsqueeze(0))
         one = keep.tile([P, 1], F32)
         nc.gpsimd.memset(one[:], 1.0)
         unused_rsqrt = keep.tile([P, 1], F32)
@@ -91,7 +94,6 @@ def tile_bdhlayer_pc_kernel(
         ident = keep.tile([P, P], F32)
         make_identity(nc, ident[:])
 
-        vectors = keep.tile([1, 2 * D], BF16)
         xs = []
         for j in range(TILES):
             xs.append(keep.tile([P, HEADS * HEAD_DIM], BF16, name="xs%d" % j))
@@ -111,8 +113,6 @@ def tile_bdhlayer_pc_kernel(
         def load_x(i):
             nc.sync.dma_start(out=x_in[i][:], in_=x_rows[:, 2 * i : 2 * i + 2, :])
 
-        nc.sync.dma_start(out=vectors[0:1, 0:D], in_=scale.unsqueeze(0))
-        nc.sync.dma_start(out=vectors[0:1, D : 2 * D], in_=running_activity.unsqueeze(0))
         for first, count in splits(0):
             load_xy(0, HEADS // PASSES * first, HEADS // PASSES * count)
         load_xy(1)

@@ -31,23 +31,11 @@ EPS_LN = 1e-5
 TARGET_ACTIVITY = 0.1
 EPS_ACTIVITY = 1e-6
 
-TRANSPOSE_AHEAD = 4
-COPY_AHEAD = 3
-QUANTISE_AHEAD = 2
-STATS_AHEAD = 1
-ADD_BEHIND = 1
-NORMALISE_BEHIND = 2
 CLOCK_RAISERS_FIRST = 20
 CLOCK_RAISERS_LATER = 4
-SCALAR_E = ()
-VECTOR_E = (5, 6, 7,)
-SCALAR_STATS = (6,)
+SCALAR_STATS_TILE = TILES - 2
 
 FLOPS = 2 * TOKENS * HEADS * HEAD_DIM * D
-
-
-def splits(j):
-    return BANK_SPLIT
 
 
 def tile_bdhlayer_pc_kernel(
@@ -71,6 +59,7 @@ def tile_bdhlayer_pc_kernel(
         vectors = keep.tile([1, 2 * D], BF16)
         nc.scalar.dma_start(out=vectors[0:1, 0:D], in_=scale.unsqueeze(0))
         nc.scalar.dma_start(out=vectors[0:1, D : 2 * D], in_=running_activity.unsqueeze(0))
+
         one = keep.tile([P, 1], F32)
         nc.gpsimd.memset(one[:], 1.0)
         unused_rsqrt = keep.tile([P, 1], F32)
@@ -113,7 +102,7 @@ def tile_bdhlayer_pc_kernel(
         def load_x(i):
             nc.sync.dma_start(out=x_in[i][:], in_=x_rows[:, 2 * i : 2 * i + 2, :])
 
-        for first, count in splits(0):
+        for first, count in BANK_SPLIT:
             load_xy(0, HEADS // PASSES * first, HEADS // PASSES * count)
         load_xy(1)
         for q in range(QUADRANTS):
@@ -168,20 +157,20 @@ def tile_bdhlayer_pc_kernel(
         planes = {}
         acc = {}
         stats = {}
-        mean_var = {}
+        mean1 = {}
+        var1 = {}
         rstd1 = {}
         centred = {}
         summed = {}
         z_sum = {}
         sq_sum = {}
-        sums1 = {}
-        neg_mean = {}
-        shift_t = {}
         rstd2 = {}
+        neg_mean2 = {}
+        shift = {}
 
         def transposes(j):
             words = xs[j][:].bitcast(F32)
-            for first, count in splits(j):
+            for first, count in BANK_SPLIT:
                 xt = psum_t.tile([P, count, 2, P], F32, name="xt%d" % count)
                 banks[(j, first)] = xt
                 for s in range(count):
@@ -195,7 +184,7 @@ def tile_bdhlayer_pc_kernel(
 
         def copy_out(j):
             grouped[j] = stage.tile([P, PASSES * K_PASS], BF16, align_bytes=64, name="grouped")
-            for first, count in splits(j):
+            for first, count in BANK_SPLIT:
                 nc.scalar.copy(
                     out=grouped[j][:]
                     .bitcast(F32)[:, PAIR_WORDS * first : PAIR_WORDS * (first + count)]
@@ -203,12 +192,10 @@ def tile_bdhlayer_pc_kernel(
                     in_=banks[(j, first)][:].rearrange("p s u r -> p s r u"),
                 )
 
-        def new_codes(j):
+        def quantise(j):
             codes[j] = stage.tile([P, PASSES * P], U32, align_bytes=64, name="codes")
             planes[j] = stage.tile([P, PASSES * P], U8, align_bytes=64, name="planes")
-
-        def quantise_part(j, part):
-            for first, count in (splits(j)[part],):
+            for first, count in BANK_SPLIT:
                 nc.vector.quantize_mx(
                     out=codes[j][:, P * first : P * (first + count)].bitcast(FP8X4),
                     scales=planes[j][:, P * first : P * (first + count)],
@@ -228,52 +215,45 @@ def tile_bdhlayer_pc_kernel(
                     stop=(g == PASSES - 1),
                 )
 
-        def scalar_first_stats(j):
-            mean_var[j] = small.tile([P, BN_AGGR_DIM], F32, name="mean_var")
-            sums1[j] = small.tile([P, 1], F32, name="sq1")
-            dump = work.tile([P, D], BF16, name="squares")
-            nc.scalar.activation(
-                out=dump[:],
-                in_=acc[j][:],
-                func=ACT.Copy,
-                scale=1.0 / D,
-                accum_out=mean_var[j][:, 0:1],
-            )
-
-        def scalar_squares(j):
-            sq1 = sums1[j]
-            dump2 = work.tile([P, D], BF16, name="squares")
-            nc.scalar.activation(
-                out=dump2[:],
-                in_=acc[j][:],
-                func=ACT.Square,
-                bias=mean_var[j][:, 0:1],
-                scale=-1.0,
-                accum_out=sq1[:],
-            )
-
         def first_stats(j):
             stats[j] = small.tile([P, BN_STATS_DIM], F32, name="stats")
             nc.vector.bn_stats(out=stats[j][:], in_=acc[j][:])
 
         def aggregate(j):
-            if j in SCALAR_STATS:
-                return
-            mean_var[j] = small.tile([P, BN_AGGR_DIM], F32, name="mean_var")
-            nc.vector.bn_aggr(out=mean_var[j][:], in_=stats[j][:])
+            mean_var = small.tile([P, BN_AGGR_DIM], F32, name="mean_var")
+            nc.vector.bn_aggr(out=mean_var[:], in_=stats[j][:])
+            mean1[j] = mean_var[:, 0:1]
+            var1[j] = mean_var[:, 1:2]
+
+        def scalar_mean(j):
+            total = small.tile([P, 1], F32, name="scalar_mean1")
+            terms = work.tile([P, D], BF16, name="terms")
+            nc.scalar.activation(
+                out=terms[:], in_=acc[j][:], func=ACT.Copy, scale=1.0 / D, accum_out=total[:]
+            )
+            mean1[j] = total[:]
+
+        def scalar_deviations(j):
+            total = small.tile([P, 1], F32, name="scalar_deviations")
+            terms = work.tile([P, D], BF16, name="terms")
+            nc.scalar.activation(
+                out=terms[:],
+                in_=acc[j][:],
+                func=ACT.Square,
+                bias=mean1[j],
+                scale=-1.0,
+                accum_out=total[:],
+            )
+            var1[j] = total[:]
 
         def first_rstd(j):
             rstd1[j] = small.tile([P, 1], F32, name="rstd1")
-            if j in SCALAR_STATS:
-                variance, factor = sums1[j][:], 1.0 / D
-            else:
-                variance, factor = mean_var[j][:, 1:2], 1.0
             nc.scalar.activation(
                 out=rstd1[j][:],
-                in_=variance,
+                in_=var1[j],
                 func=ACT.Abs_reciprocal_sqrt,
                 bias=EPS_LN,
-                scale=factor,
+                scale=1.0 / D if j == SCALAR_STATS_TILE else 1.0,
             )
 
         def centre_and_gain(j):
@@ -281,7 +261,7 @@ def tile_bdhlayer_pc_kernel(
             nc.vector.scalar_tensor_tensor(
                 out=centred[j][:],
                 in0=acc[j][:],
-                scalar=mean_var[j][:, 0:1],
+                scalar=mean1[j],
                 in1=gain[:],
                 op0=ALU.subtract,
                 op1=ALU.mult,
@@ -301,15 +281,21 @@ def tile_bdhlayer_pc_kernel(
             )
 
         def sum_squares(j):
-            squares = work.tile([P, D], BF16, name="squares")
+            terms = work.tile([P, D], BF16, name="terms")
             sq_sum[j] = small.tile([P, 1], F32, name="sq_sum")
             nc.scalar.activation(
-                out=squares[:],
+                out=terms[:],
                 in_=summed[j][:],
                 func=ACT.Square,
                 bias=z_sum[j][:, 0:1],
                 scale=-1.0 * D,
                 accum_out=sq_sum[j][:],
+            )
+
+        def negate_mean(j):
+            neg_mean2[j] = small.tile([P, 1], F32, name="neg_mean2")
+            nc.scalar.activation(
+                out=neg_mean2[j][:], in_=z_sum[j][:], func=ACT.Copy, scale=-1.0 / D
             )
 
         def second_rstd(j):
@@ -322,98 +308,62 @@ def tile_bdhlayer_pc_kernel(
                 scale=1.0 / (D * D * D),
             )
 
-        def negate_mean(j):
-            neg_mean[j] = small.tile([P, 1], F32, name="neg_mean")
-            nc.vector.tensor_scalar_mul(out=neg_mean[j][:], in0=z_sum[j][:], scalar1=-1.0 / D)
-
-        def normalise(j):
-            result = work.tile([P, D], F32, name="result")
-            engine = nc.vector if j in VECTOR_E else nc.gpsimd
-            engine.tensor_scalar(
-                out=result[:],
-                in0=summed[j][:],
-                scalar1=neg_mean[j][:, 0:1],
-                scalar2=rstd2[j][:, 0:1],
-                op0=ALU.add,
-                op1=ALU.mult,
+        def make_shift(j):
+            shift[j] = small.tile([P, 1], F32, name="shift")
+            nc.scalar.activation(
+                out=shift[j][:], in_=neg_mean2[j][:], func=ACT.Copy, scale=rstd2[j][:, 0:1]
             )
+
+        def store(j, result):
             nc.sync.dma_start(out=out_rows[:, j, :], in_=result[:])
 
-        def scalar_negate(j):
-            neg_mean[j] = small.tile([P, 1], F32, name="neg_mean_s")
-            nc.scalar.activation(out=neg_mean[j][:], in_=z_sum[j][:], func=ACT.Copy, scale=-1.0 / D)
-
-        def shift_of(j):
-            shift_t[j] = small.tile([P, 1], F32, name="shift_t")
-            nc.scalar.activation(
-                out=shift_t[j][:], in_=neg_mean[j][:], func=ACT.Copy, scale=rstd2[j][:, 0:1]
-            )
-
-        def pool_normalise(j):
+        def gpsimd_normalise(j):
             result = work.tile([P, D], F32, name="result")
             nc.gpsimd.tensor_scalar(
                 out=result[:],
                 in0=summed[j][:],
                 scalar1=rstd2[j][:, 0:1],
-                scalar2=shift_t[j][:, 0:1],
+                scalar2=shift[j][:, 0:1],
                 op0=ALU.mult,
                 op1=ALU.add,
             )
-            nc.sync.dma_start(out=out_rows[:, j, :], in_=result[:])
+            store(j, result)
 
-        def scalar_apply(j):
+        def scalar_normalise(j):
             result = work.tile([P, D], F32, name="result")
             nc.scalar.activation(
                 out=result[:],
                 in_=summed[j][:],
                 func=ACT.Identity,
-                bias=shift_t[j][:, 0:1],
+                bias=shift[j][:, 0:1],
                 scale=rstd2[j][:, 0:1],
             )
-            nc.sync.dma_start(out=out_rows[:, j, :], in_=result[:])
+            store(j, result)
 
-        def scalar_normalise_and_store(j):
-            neg_mean2 = small.tile([P, 1], F32, name="neg_mean2")
-            nc.scalar.activation(
-                out=neg_mean2[:], in_=z_sum[j][:], func=ACT.Copy, scale=-1.0 / D
-            )
-            shift = small.tile([P, 1], F32, name="shift")
-            nc.scalar.activation(
-                out=shift[:], in_=neg_mean2[:], func=ACT.Copy, scale=rstd2[j][:, 0:1]
-            )
+        def vector_normalise(j):
             result = work.tile([P, D], F32, name="result")
-            nc.scalar.activation(
+            nc.vector.tensor_scalar(
                 out=result[:],
-                in_=summed[j][:],
-                func=ACT.Identity,
-                bias=shift[:, 0:1],
-                scale=rstd2[j][:, 0:1],
+                in0=summed[j][:],
+                scalar1=neg_mean2[j][:, 0:1],
+                scalar2=rstd2[j][:, 0:1],
+                op0=ALU.add,
+                op1=ALU.mult,
             )
-            nc.sync.dma_start(out=out_rows[:, j, :], in_=result[:])
-
-        def by_scalar(j):
-            return j in SCALAR_E
-
-        def live(j):
-            return 0 <= j < TILES
+            store(j, result)
 
         transposes(0)
         spread_vectors()
-        raise_clock(4)
         transposes(1)
-        raise_clock(4)
+        raise_clock(CLOCK_RAISERS_LATER)
         copy_out(0)
         regulate()
-        new_codes(0)
-        for part in range(len(splits(0))):
-            quantise_part(0, part)
+        quantise(0)
         multiply(0)
         transposes(2)
         copy_out(1)
         build_gain()
-        new_codes(1)
-        for part in range(len(splits(1))):
-            quantise_part(1, part)
+        quantise(1)
         multiply(1)
         transposes(3)
         copy_out(2)
@@ -421,69 +371,58 @@ def tile_bdhlayer_pc_kernel(
         aggregate(0)
         first_rstd(0)
         centre_and_gain(0)
-        new_codes(2)
-        for part in range(len(splits(2))):
-            quantise_part(2, part)
+        quantise(2)
         multiply(2)
         transposes(4)
         copy_out(3)
         first_stats(1)
-        for j in range(1, 6):
-            if j + 1 in SCALAR_STATS:
-                scalar_first_stats(j + 1)
-            if live(j - 1):
-                add_tokens(j - 1)
-            if live(j) and j not in SCALAR_STATS:
-                aggregate(j)
-            if live(j):
-                first_rstd(j)
-            if live(j - 2):
-                shift_of(j - 2)
-            if j + 1 in SCALAR_STATS:
-                scalar_squares(j + 1)
-            if live(j - 1):
-                sum_squares(j - 1)
-            if live(j + 3):
+
+        for j in range(1, TILES - 2):
+            if j + 1 == SCALAR_STATS_TILE:
+                scalar_mean(j + 1)
+            add_tokens(j - 1)
+            aggregate(j)
+            first_rstd(j)
+            if j >= 2:
+                make_shift(j - 2)
+            if j + 1 == SCALAR_STATS_TILE:
+                scalar_deviations(j + 1)
+            sum_squares(j - 1)
+            if j + 3 < TILES:
                 copy_out(j + 3)
-            if live(j - 1):
-                scalar_negate(j - 1)
-            if live(j - 1):
-                second_rstd(j - 1)
-            if live(j + 2):
-                new_codes(j + 2)
-                quantise_part(j + 2, 0)
-            if live(j + 2):
-                quantise_part(j + 2, 1)
-            if live(j + 2):
+            negate_mean(j - 1)
+            second_rstd(j - 1)
+            if j + 2 < TILES:
+                quantise(j + 2)
                 multiply(j + 2)
-            if live(j + 4):
+            if j + 4 < TILES:
                 transposes(j + 4)
-            if live(j - 2):
-                pool_normalise(j - 2)
-            if live(j):
-                centre_and_gain(j)
-            if live(j + 1) and j + 1 not in SCALAR_STATS:
+            if j >= 2:
+                gpsimd_normalise(j - 2)
+            centre_and_gain(j)
+            if j + 1 != SCALAR_STATS_TILE:
                 first_stats(j + 1)
+
         first_rstd(6)
-        shift_of(4)
+        make_shift(4)
         centre_and_gain(6)
         first_stats(7)
         add_tokens(5)
-        scalar_apply(4)
+        scalar_normalise(4)
         sum_squares(5)
-        scalar_negate(5)
+        negate_mean(5)
         second_rstd(5)
         aggregate(7)
         first_rstd(7)
         add_tokens(6)
         sum_squares(6)
-        scalar_negate(6)
+        negate_mean(6)
         centre_and_gain(7)
         second_rstd(6)
         add_tokens(7)
         sum_squares(7)
-        second_rstd(7)
-        normalise(5)
         negate_mean(7)
-        normalise(6)
-        normalise(7)
+        second_rstd(7)
+        vector_normalise(5)
+        vector_normalise(6)
+        vector_normalise(7)

@@ -31,8 +31,7 @@ EPS_LN = 1e-5
 TARGET_ACTIVITY = 0.1
 EPS_ACTIVITY = 1e-6
 
-CLOCK_RAISERS_FIRST = 20
-CLOCK_RAISERS_LATER = 4
+CLOCK_RAISERS = 20
 SCALAR_STATS_TILE = TILES - 2
 
 FLOPS = 2 * TOKENS * HEADS * HEAD_DIM * D
@@ -75,11 +74,8 @@ def tile_bdhlayer_pc_kernel(
         nc.gpsimd.memset(zeros[:], 0.0)
         unread = psum_idle.tile([P, P], F32, name="unread")
 
-        def raise_clock(times):
-            for i in range(times):
-                nc.tensor.matmul(unread[:], lhsT=zeros[:], rhs=zeros[:], start=True, stop=True)
-
-        raise_clock(CLOCK_RAISERS_FIRST)
+        for i in range(CLOCK_RAISERS):
+            nc.tensor.matmul(unread[:], lhsT=zeros[:], rhs=zeros[:], start=True, stop=True)
         ident = keep.tile([P, P], F32)
         make_identity(nc, ident[:])
 
@@ -355,7 +351,6 @@ def tile_bdhlayer_pc_kernel(
         transposes(0)
         spread_vectors()
         transposes(1)
-        raise_clock(CLOCK_RAISERS_LATER)
         copy_out(0)
         regulate()
         quantise(0)

@@ -23,6 +23,7 @@ PASSES = HEADS * HEAD_DIM // K_PASS
 TILES = TOKENS // P
 PAIR_WORDS = K_PASS // 2
 BANK_SPLIT = ((0, 2), (2, 1))
+WORD_SPLIT = ((0, 2), (2, 1))
 QUADRANTS = 4
 SCALE_ROWS = 4
 BN_STATS_DIM = 6
@@ -87,19 +88,18 @@ def tile_bdhlayer_pc_kernel(
             x_in.append(keep.tile([P, 2, D], BF16, name="x_in%d" % i))
         w_words = keep.tile([P, PASSES, 2 * D], U8, align_bytes=64)
 
-        def load_xy(j, first_head=0, heads=HEADS):
-            nc.sync.dma_start(
-                out=xs[j][:].rearrange("p (h n) -> p h n", h=HEADS)[
-                    :, first_head : first_head + heads, :
-                ],
-                in_=xy_tiles[j][:, first_head : first_head + heads, :],
-            )
+        def load_xy(j, split=((0, PASSES),)):
+            for first, count in split:
+                heads = slice(HEADS // PASSES * first, HEADS // PASSES * (first + count))
+                nc.sync.dma_start(
+                    out=xs[j][:].rearrange("p (h n) -> p h n", h=HEADS)[:, heads, :],
+                    in_=xy_tiles[j][:, heads, :],
+                )
 
         def load_x(i):
             nc.sync.dma_start(out=x_in[i][:], in_=x_rows[:, 2 * i : 2 * i + 2, :])
 
-        for first, count in BANK_SPLIT:
-            load_xy(0, HEADS // PASSES * first, HEADS // PASSES * count)
+        load_xy(0, BANK_SPLIT)
         load_xy(1)
         for q in range(QUADRANTS):
             nc.sync.dma_start(
@@ -108,11 +108,15 @@ def tile_bdhlayer_pc_kernel(
                     :, SCALE_ROWS * q : SCALE_ROWS * (q + 1), :
                 ].rearrange("g r w -> r g w"),
             )
-        nc.sync.dma_start(
-            out=w_words[:].bitcast(I32),
-            in_=decoder_words.bitcast(I32).rearrange("g p w -> p g w"),
-        )
-        for i in range(1, TILES // 2):
+        for first, count in WORD_SPLIT:
+            nc.sync.dma_start(
+                out=w_words[:, first : first + count, :].bitcast(I32),
+                in_=decoder_words[first : first + count].bitcast(I32).rearrange("g p w -> p g w"),
+            )
+        load_xy(2, BANK_SPLIT)
+        load_xy(3)
+        load_x(0)
+        for i in range(2, TILES // 2):
             load_xy(2 * i)
             load_xy(2 * i + 1)
             load_x(i - 1)

from contextlib import ExitStack

import concourse.mybir as mybir
from concourse.masks import make_identity

F32 = mybir.dt.float32
BF16 = mybir.dt.bfloat16
I32 = mybir.dt.int32
U32 = mybir.dt.uint32
U8 = mybir.dt.uint8
FP8X4 = mybir.dt.float8_e4m3fn_x4
FP4X4 = mybir.dt.float4_e2m1fn_x4
ALU = mybir.AluOpType
ACT = mybir.ActivationFunctionType

P = 128
HEADS = 6
HEAD_DIM = 256
TOKENS = 1024
D = 512
K_PASS = 512
PASSES = HEADS * HEAD_DIM // K_PASS
TILES = TOKENS // P
PAIR_WORDS = K_PASS // 2
BANK_SPLIT = ((0, 2), (2, 1))
WORD_SPLIT = ((0, 2), (2, 1))
QUADRANTS = 4
SCALE_ROWS = 4
BN_STATS_DIM = 6
BN_AGGR_DIM = 2
EPS_LN = 1e-5
TARGET_ACTIVITY = 0.1
EPS_ACTIVITY = 1e-6

CLOCK_RAISERS = 20
SCALAR_STATS_TILE = TILES - 2

FLOPS = 2 * TOKENS * HEADS * HEAD_DIM * D


def tile_bdhlayer_pc_kernel(
    tc, xy_sparse, decoder_words, decoder_scales, x, scale, running_activity, out
):
    nc = tc.nc
    xy_tiles = xy_sparse.rearrange("b h (p j) n -> j p (b h) n", j=TILES)
    x_rows = x.rearrange("a b (p j) n -> p (a b j) n", j=TILES)
    out_rows = out.rearrange("a b (p j) n -> p (a b j) n", j=TILES)

    with ExitStack() as ctx:
        keep = ctx.enter_context(tc.tile_pool(name="keep", bufs=1))
        stage = ctx.enter_context(tc.tile_pool(name="stage", bufs=4))
        work = ctx.enter_context(tc.tile_pool(name="work", bufs=4))
        small = ctx.enter_context(tc.tile_pool(name="small", bufs=4))
        psum_t = ctx.enter_context(tc.psum_pool(name="psum_t", bufs=2))
        psum_acc = ctx.enter_context(tc.psum_pool(name="psum_acc", bufs=3))
        psum_idle = ctx.enter_context(tc.psum_pool(name="psum_idle", bufs=1))
        ctx.enter_context(tc.manual_schedule())

        vectors = keep.tile([1, 2 * D], BF16)
        nc.scalar.dma_start(out=vectors[0:1, 0:D], in_=scale.unsqueeze(0))
        nc.scalar.dma_start(out=vectors[0:1, D : 2 * D], in_=running_activity.unsqueeze(0))

        one = keep.tile([P, 1], F32)
        nc.gpsimd.memset(one[:], 1.0)
        unused_rsqrt = keep.tile([P, 1], F32)
        nc.scalar.activation(out=unused_rsqrt[:], in_=one[:], func=ACT.Abs_reciprocal_sqrt)

        w_planes = keep.tile([P, PASSES, D], U8, align_bytes=64)
        nc.vector.memset(w_planes[:].bitcast(I32), 0)
        padded = keep.tile([P, 2 * D], BF16)
        nc.vector.memset(padded[:], 0.0)
        ones = keep.tile([P, P], BF16)
        nc.vector.memset(ones[:], 1.0)
        zeros = keep.tile([P, P], BF16)
        nc.gpsimd.memset(zeros[:], 0.0)
        unread = psum_idle.tile([P, P], F32, name="unread")

        for i in range(CLOCK_RAISERS):
            nc.tensor.matmul(unread[:], lhsT=zeros[:], rhs=zeros[:], start=True, stop=True)
        ident = keep.tile([P, P], F32)
        make_identity(nc, ident[:])

        xs = []
        for j in range(TILES):
            xs.append(keep.tile([P, HEADS * HEAD_DIM], BF16, name="xs%d" % j))
        x_in = []
        for i in range(TILES // 2):
            x_in.append(keep.tile([P, 2, D], BF16, name="x_in%d" % i))
        w_words = keep.tile([P, PASSES, 2 * D], U8, align_bytes=64)

        def load_xy(j, split=((0, PASSES),)):
            for first, count in split:
                heads = slice(HEADS // PASSES * first, HEADS // PASSES * (first + count))
                nc.sync.dma_start(
                    out=xs[j][:].rearrange("p (h n) -> p h n", h=HEADS)[:, heads, :],
                    in_=xy_tiles[j][:, heads, :],
                )

        def load_x(i):
            nc.sync.dma_start(out=x_in[i][:], in_=x_rows[:, 2 * i : 2 * i + 2, :])

        load_xy(0, BANK_SPLIT)
        load_xy(1)
        for q in range(QUADRANTS):
            nc.sync.dma_start(
                out=w_planes[32 * q : 32 * q + SCALE_ROWS].bitcast(I32),
                in_=decoder_scales.bitcast(I32)[
                    :, SCALE_ROWS * q : SCALE_ROWS * (q + 1), :
                ].rearrange("g r w -> r g w"),
            )
        for first, count in WORD_SPLIT:
            nc.sync.dma_start(
                out=w_words[:, first : first + count, :].bitcast(I32),
                in_=decoder_words[first : first + count].bitcast(I32).rearrange("g p w -> p g w"),
            )
        load_xy(2, BANK_SPLIT)
        load_xy(3)
        load_x(0)
        for i in range(2, TILES // 2):
            load_xy(2 * i)
            load_xy(2 * i + 1)
            load_x(i - 1)
        load_x(TILES // 2 - 1)

        nc.vector.tensor_copy(out=padded[0:1, :], in_=vectors[0:1, :])
        regulation = keep.tile([P, D], F32)
        gain = keep.tile([P, D], F32)
        spread = {}

        def spread_vectors():
            spread["scale"] = psum_acc.tile([P, D], F32, name="acc")
            nc.tensor.matmul(
                spread["scale"][:], lhsT=ones[:], rhs=padded[:, 0:D], start=True, stop=True
            )
            spread["activity"] = psum_acc.tile([P, D], F32, name="acc")
            nc.tensor.matmul(
                spread["activity"][:], lhsT=ones[:], rhs=padded[:, D : 2 * D], start=True, stop=True
            )

        def regulate():
            nc.scalar.activation(
                out=regulation[:],
                in_=spread["activity"][:],
                func=ACT.Abs_reciprocal_sqrt,
                bias=EPS_ACTIVITY / TARGET_ACTIVITY,
                scale=1.0 / TARGET_ACTIVITY,
            )

        def build_gain():
            nc.vector.tensor_tensor(
                out=gain[:], in0=regulation[:], in1=spread["scale"][:], op=ALU.mult
            )

        banks = {}
        grouped = {}
        codes = {}
        planes = {}
        acc = {}
        stats = {}
        mean1 = {}
        var1 = {}
        rstd1 = {}
        centred = {}
        summed = {}
        z_sum = {}
        sq_sum = {}
        rstd2 = {}
        neg_mean2 = {}
        shift = {}

        def transposes(j):
            words = xs[j][:].bitcast(F32)
            for first, count in BANK_SPLIT:
                xt = psum_t.tile([P, count, 2, P], F32, name="xt%d" % count)
                banks[(j, first)] = xt
                for s in range(count):
                    g = first + s
                    for u in range(2):
                        nc.tensor.transpose(
                            xt[:, s, u, :],
                            words[:, PAIR_WORDS * g + u : PAIR_WORDS * (g + 1) : 2],
                            ident[:],
                        )

        def copy_out(j):
            grouped[j] = stage.tile([P, PASSES * K_PASS], BF16, align_bytes=64, name="grouped")
            for first, count in BANK_SPLIT:
                nc.scalar.copy(
                    out=grouped[j][:]
                    .bitcast(F32)[:, PAIR_WORDS * first : PAIR_WORDS * (first + count)]
                    .rearrange("p (s r u) -> p s r u", s=count, u=2),
                    in_=banks[(j, first)][:].rearrange("p s u r -> p s r u"),
                )

        def quantise(j):
            codes[j] = stage.tile([P, PASSES * P], U32, align_bytes=64, name="codes")
            planes[j] = stage.tile([P, PASSES * P], U8, align_bytes=64, name="planes")
            for first, count in BANK_SPLIT:
                nc.vector.quantize_mx(
                    out=codes[j][:, P * first : P * (first + count)].bitcast(FP8X4),
                    scales=planes[j][:, P * first : P * (first + count)],
                    in_=grouped[j][:, K_PASS * first : K_PASS * (first + count)],
                )

        def multiply(j):
            acc[j] = psum_acc.tile([P, D], F32, name="acc")
            for g in range(PASSES):
                nc.tensor.matmul_mx(
                    out=acc[j][:],
                    lhsT=codes[j][:, P * g : P * (g + 1)].bitcast(FP8X4),
                    lhsT_scale=planes[j][:, P * g : P * (g + 1)],
                    rhs=w_words[:, g, :].bitcast(FP4X4),
                    rhs_scale=w_planes[:, g, :],
                    start=(g == 0),
                    stop=(g == PASSES - 1),
                )

        def first_stats(j):
            stats[j] = small.tile([P, BN_STATS_DIM], F32, name="stats")
            nc.vector.bn_stats(out=stats[j][:], in_=acc[j][:])

        def aggregate(j):
            mean_var = small.tile([P, BN_AGGR_DIM], F32, name="mean_var")
            nc.vector.bn_aggr(out=mean_var[:], in_=stats[j][:])
            mean1[j] = mean_var[:, 0:1]
            var1[j] = mean_var[:, 1:2]

        def scalar_mean(j):
            total = small.tile([P, 1], F32, name="scalar_mean1")
            terms = work.tile([P, D], BF16, name="terms")
            nc.scalar.activation(
                out=terms[:], in_=acc[j][:], func=ACT.Copy, scale=1.0 / D, accum_out=total[:]
            )
            mean1[j] = total[:]

        def scalar_deviations(j):
            total = small.tile([P, 1], F32, name="scalar_deviations")
            terms = work.tile([P, D], BF16, name="terms")
            nc.scalar.activation(
                out=terms[:],
                in_=acc[j][:],
                func=ACT.Square,
                bias=mean1[j],
                scale=-1.0,
                accum_out=total[:],
            )
            var1[j] = total[:]

        def first_rstd(j):
            rstd1[j] = small.tile([P, 1], F32, name="rstd1")
            nc.scalar.activation(
                out=rstd1[j][:],
                in_=var1[j],
                func=ACT.Abs_reciprocal_sqrt,
                bias=EPS_LN,
                scale=1.0 / D if j == SCALAR_STATS_TILE else 1.0,
            )

        def centre_and_gain(j):
            centred[j] = work.tile([P, D], F32, name="centred")
            nc.vector.scalar_tensor_tensor(
                out=centred[j][:],
                in0=acc[j][:],
                scalar=mean1[j],
                in1=gain[:],
                op0=ALU.subtract,
                op1=ALU.mult,
            )

        def add_tokens(j):
            summed[j] = work.tile([P, D], F32, name="summed")
            z_sum[j] = small.tile([P, 1], F32, name="z_sum")
            nc.vector.scalar_tensor_tensor(
                out=summed[j][:],
                in0=centred[j][:],
                scalar=rstd1[j][:, 0:1],
                in1=x_in[j // 2][:, j % 2, :],
                op0=ALU.mult,
                op1=ALU.add,
                accum_out=z_sum[j][:],
            )

        def sum_squares(j):
            terms = work.tile([P, D], BF16, name="terms")
            sq_sum[j] = small.tile([P, 1], F32, name="sq_sum")
            nc.scalar.activation(
                out=terms[:],
                in_=summed[j][:],
                func=ACT.Square,
                bias=z_sum[j][:, 0:1],
                scale=-1.0 * D,
                accum_out=sq_sum[j][:],
            )

        def negate_mean(j):
            neg_mean2[j] = small.tile([P, 1], F32, name="neg_mean2")
            nc.scalar.activation(
                out=neg_mean2[j][:], in_=z_sum[j][:], func=ACT.Copy, scale=-1.0 / D
            )

        def second_rstd(j):
            rstd2[j] = small.tile([P, 1], F32, name="rstd2")
            nc.scalar.activation(
                out=rstd2[j][:],
                in_=sq_sum[j][:],
                func=ACT.Abs_reciprocal_sqrt,
                bias=EPS_LN,
                scale=1.0 / (D * D * D),
            )

        def make_shift(j):
            shift[j] = small.tile([P, 1], F32, name="shift")
            nc.scalar.activation(
                out=shift[j][:], in_=neg_mean2[j][:], func=ACT.Copy, scale=rstd2[j][:, 0:1]
            )

        def store(j, result):
            nc.sync.dma_start(out=out_rows[:, j, :], in_=result[:])

        def gpsimd_normalise(j):
            result = work.tile([P, D], F32, name="result")
            nc.gpsimd.tensor_scalar(
                out=result[:],
                in0=summed[j][:],
                scalar1=rstd2[j][:, 0:1],
                scalar2=shift[j][:, 0:1],
                op0=ALU.mult,
                op1=ALU.add,
            )
            store(j, result)

        def scalar_normalise(j):
            result = work.tile([P, D], F32, name="result")
            nc.scalar.activation(
                out=result[:],
                in_=summed[j][:],
                func=ACT.Identity,
                bias=shift[j][:, 0:1],
                scale=rstd2[j][:, 0:1],
            )
            store(j, result)

        def vector_normalise(j):
            result = work.tile([P, D], F32, name="result")
            nc.vector.tensor_scalar(
                out=result[:],
                in0=summed[j][:],
                scalar1=neg_mean2[j][:, 0:1],
                scalar2=rstd2[j][:, 0:1],
                op0=ALU.add,
                op1=ALU.mult,
            )
            store(j, result)

        transposes(0)
        spread_vectors()
        transposes(1)
        copy_out(0)
        regulate()
        quantise(0)
        multiply(0)
        transposes(2)
        copy_out(1)
        build_gain()
        quantise(1)
        multiply(1)
        transposes(3)
        copy_out(2)
        first_stats(0)
        aggregate(0)
        first_rstd(0)
        centre_and_gain(0)
        quantise(2)
        multiply(2)
        transposes(4)
        copy_out(3)
        first_stats(1)

        for j in range(1, TILES - 2):
            if j + 1 == SCALAR_STATS_TILE:
                scalar_mean(j + 1)
            add_tokens(j - 1)
            aggregate(j)
            first_rstd(j)
            if j >= 2:
                make_shift(j - 2)
            if j + 1 == SCALAR_STATS_TILE:
                scalar_deviations(j + 1)
            sum_squares(j - 1)
            if j + 3 < TILES:
                copy_out(j + 3)
            negate_mean(j - 1)
            second_rstd(j - 1)
            if j + 2 < TILES:
                quantise(j + 2)
                multiply(j + 2)
            if j + 4 < TILES:
                transposes(j + 4)
            if j >= 2:
                gpsimd_normalise(j - 2)
            centre_and_gain(j)
            if j + 1 != SCALAR_STATS_TILE:
                first_stats(j + 1)

        first_rstd(6)
        make_shift(4)
        centre_and_gain(6)
        first_stats(7)
        add_tokens(5)
        scalar_normalise(4)
        sum_squares(5)
        negate_mean(5)
        second_rstd(5)
        aggregate(7)
        first_rstd(7)
        add_tokens(6)
        sum_squares(6)
        negate_mean(6)
        centre_and_gain(7)
        second_rstd(6)
        add_tokens(7)
        sum_squares(7)
        negate_mean(7)
        second_rstd(7)
        vector_normalise(5)
        vector_normalise(6)
        vector_normalise(7)
